import numpy as np
import ml_dtypes


def mxq(x, axis, fmt="e4m3"):
    dtype, down = {"e4m3": (ml_dtypes.float8_e4m3fn, 7), "e5m2": (ml_dtypes.float8_e5m2, 14)}[fmt]
    v = np.moveaxis(np.asarray(x, np.float32).astype(ml_dtypes.bfloat16).astype(np.float64), axis, -1)
    blocks = v.reshape(v.shape[:-1] + (-1, 32))
    amax = np.abs(blocks).max(-1, keepdims=True)
    byte = np.maximum(np.where(amax > 0, np.frexp(amax)[1] - 1 + 127, 0) - down, 1)
    scale = np.exp2(byte - 127.0)
    codes = (blocks / scale).astype(np.float32).astype(dtype).astype(np.float64)
    return np.moveaxis((codes * scale).reshape(v.shape), -1, axis)


WIDE = False


def mx_kscale(k):
    if not WIDE:
        return np.ones(k)
    levels = np.array([10, -10, 5, -5, 0])
    a = np.random.permutation(np.resize(levels, k // 512 * 4)).reshape(k // 512, 4)
    idx = np.arange(k)
    return np.exp2(a[idx // 512, idx % 128 // 32])


BF16 = ml_dtypes.bfloat16


def bf(x):
    return np.asarray(x, np.float32).astype(BF16)


def f64(x):
    return np.asarray(x).astype(np.float64)


E2M1 = np.array([0.0, 0.5, 1.0, 1.5, 2.0, 3.0, 4.0, 6.0, -0.0, -0.5, -1.0, -1.5, -2.0, -3.0, -4.0, -6.0])


def pack_weight(w, fmt):
    k, n = w.shape
    w = f64(bf(w)).reshape(k // 32, 32, n)
    amax = np.abs(w).max(1)
    if fmt == "e4m3":
        byte = np.frexp(amax)[1] - 1 + 127 - 7
    else:
        mant, ex = np.frexp(amax / 6.0)
        byte = np.where(mant > 0.5, ex, ex - 1) + 127
    byte = np.clip(np.where(amax > 0, byte, 1), 1, 254)
    scaled = (w * np.exp2(127.0 - byte)[:, None, :]).reshape(k, n).astype(np.float32)
    by_word = np.ascontiguousarray(scaled.reshape(k // 512, 128, 4, n).transpose(0, 1, 3, 2))
    if fmt == "e4m3":
        words = by_word.astype(ml_dtypes.float8_e4m3fn).view(np.uint8)
    else:
        c = by_word.astype(ml_dtypes.float4_e2m1fn).view(np.uint8) & 0xF
        words = c[..., 0::2] | (c[..., 1::2] << 4)
    return np.ascontiguousarray(words), np.ascontiguousarray(byte.astype(np.uint8).reshape(k // 512, 16, n))


def unpack_weight(words, scales, fmt):
    g, p, n, _ = words.shape
    if fmt == "e4m3":
        vals = np.ascontiguousarray(words).view(ml_dtypes.float8_e4m3fn).astype(np.float64)
    else:
        nib = np.empty((g, p, n, 4), np.uint8)
        nib[..., 0::2] = words & 0xF
        nib[..., 1::2] = words >> 4
        vals = E2M1[nib]
    vals = vals * np.repeat(np.exp2(scales.astype(np.float64) - 127.0), 8, axis=1)[..., None]
    return vals.transpose(0, 1, 3, 2).reshape(g * 512, n)


B, I, H = 128, 8192, 512
FORGET_GATE_BIAS = -1.0
EPS = 1e-5
FMT = "e4m3"


def sigmoid(v):
    return 1.0 / (1.0 + np.exp(-v))


def layer_norm_1d(x, weight, bias):
    mean = np.mean(x, axis=1, keepdims=True)
    std = np.std(x, axis=1, keepdims=True, ddof=1)
    return (x - mean) / (std + EPS) * weight + bias


def setup_inputs():
    s, t = mx_kscale(I), mx_kscale(H)
    inputs = bf(np.random.standard_normal((B, I)) * s)
    hx = bf(np.random.standard_normal((B, H)) * t)
    cx = bf(np.random.standard_normal((B, H)))
    w_i2h = np.random.standard_normal((4 * H, I)) / np.sqrt(I) / s
    w_i2h_words, w_i2h_scales = pack_weight(np.ascontiguousarray(w_i2h.T), FMT)
    b_i2h = bf(np.random.standard_normal(4 * H) * 0.3)
    w_h2h = np.random.standard_normal((4 * H, H)) / np.sqrt(H) / t
    w_h2h_words, w_h2h_scales = pack_weight(np.ascontiguousarray(w_h2h.T), FMT)
    b_h2h = bf(np.random.standard_normal(4 * H) * 0.3)
    return {
        "inputs": inputs,
        "hx": hx,
        "cx": cx,
        "w_i2h_words": w_i2h_words,
        "w_i2h_scales": w_i2h_scales,
        "b_i2h": b_i2h,
        "w_h2h_words": w_h2h_words,
        "w_h2h_scales": w_h2h_scales,
        "b_h2h": b_h2h,
        "ln_i2h_w": bf(1.0 + 0.2 * np.random.standard_normal((1, 4 * H))),
        "ln_i2h_b": bf(0.2 * np.random.standard_normal((1, 4 * H))),
        "ln_h2h_w": bf(1.0 + 0.2 * np.random.standard_normal((1, 4 * H))),
        "ln_h2h_b": bf(0.2 * np.random.standard_normal((1, 4 * H))),
        "ln_h2o_w": bf(1.0 + 0.2 * np.random.standard_normal((1, H))),
        "ln_h2o_b": bf(0.2 * np.random.standard_normal((1, H))),
    }


def reference(inputs, hx, cx, w_i2h_words, w_i2h_scales, b_i2h, w_h2h_words, w_h2h_scales, b_h2h,
              ln_i2h_w, ln_i2h_b, ln_h2h_w, ln_h2h_b, ln_h2o_w, ln_h2o_b):
    i2h = (mxq(f64(inputs), 1, "e4m3") @ unpack_weight(w_i2h_words, w_i2h_scales, FMT)) + f64(b_i2h)
    h2h = (mxq(f64(hx), 1, "e4m3") @ unpack_weight(w_h2h_words, w_h2h_scales, FMT)) + f64(b_h2h)
    x = layer_norm_1d(i2h, f64(ln_i2h_w), f64(ln_i2h_b)) + layer_norm_1d(h2h, f64(ln_h2h_w), f64(ln_h2h_b))
    g_i, g_f, g_o, g_c = np.split(x, 4, axis=1)
    in_gate = sigmoid(g_i)
    forget_gate = sigmoid(g_f + FORGET_GATE_BIAS)
    out_gate = sigmoid(g_o)
    in_transform = np.tanh(g_c)
    cx_new = forget_gate * f64(cx) + in_gate * in_transform
    hx_new = out_gate * np.tanh(layer_norm_1d(cx_new, f64(ln_h2o_w), f64(ln_h2o_b)))
    return hx_new, cx_new

@@ -1,0 +1,314 @@
+import math
+from contextlib import ExitStack
+
+import concourse.mybir as mybir
+from concourse.masks import make_identity
+
+F32 = mybir.dt.float32
+BF16 = mybir.dt.bfloat16
+I32 = mybir.dt.int32
+U32 = mybir.dt.uint32
+U8 = mybir.dt.uint8
+FP8X4 = mybir.dt.float8_e4m3fn_x4
+ALU = mybir.AluOpType
+ACT = mybir.ActivationFunctionType
+
+P = 128
+PACK = 4
+K_PASS = P * PACK
+IN = 8192
+HID = 512
+GATES = 4
+WIDE = GATES * HID
+GATE_I = 0
+GATE_F = 1
+GATE_O = 2
+GATE_C = 3
+FORGET_GATE_BIAS = -1.0
+EPS = 1e-5
+
+X_GROUPS = IN // K_PASS
+H_GROUP = X_GROUPS
+GROUPS = X_GROUPS + 1
+CHUNK = 4
+PLANES = 4
+LAST = 4
+MAIN = X_GROUPS - LAST
+
+ROW_B_I2H = 0
+ROW_W_I2H = 1
+ROW_S_I2H = 2
+ROW_S_H2H = 3
+ROW_B_H2H = 4
+ROW_W_H2H = 5
+ROW_H2O = 6
+
+FLOPS = 2 * P * (IN + HID) * WIDE
+
+
+def mean_and_rstd(nc, small, stats, count, half, label):
+    mean_var = small.tile([P, 2], F32, name="mean_var_" + label)
+    nc.vector.bn_aggr(out=mean_var[:], in_=stats)
+    root = small.tile([P, 1], F32, name="root_" + label)
+    nc.gpsimd.tensor_tensor(out=root[:], in0=mean_var[:, 1:2], in1=half[:], op=ALU.pow)
+    std_eps = small.tile([P, 1], F32, name="std_eps_" + label)
+    nc.vector.tensor_scalar(
+        out=std_eps[:],
+        in0=root[:],
+        scalar1=math.sqrt(count / (count - 1.0)),
+        scalar2=EPS,
+        op0=ALU.mult,
+        op1=ALU.add,
+    )
+    rstd = small.tile([P, 1], F32, name="rstd_" + label)
+    nc.vector.reciprocal(out=rstd[:], in_=std_eps[:])
+    return mean_var[:, 0:1], rstd[:]
+
+
+def centre_times_gain(nc, out, value, mean, gain):
+    nc.vector.scalar_tensor_tensor(
+        out=out, in0=value, scalar=mean, in1=gain, op0=ALU.subtract, op1=ALU.mult
+    )
+
+
+def scale_plus_shift(nc, out, value, rstd, shift):
+    nc.vector.scalar_tensor_tensor(
+        out=out, in0=value, scalar=rstd, in1=shift, op0=ALU.mult, op1=ALU.add
+    )
+
+
+def tile_layernormlstmcell_k_kernel(
+    tc,
+    inputs,
+    hx,
+    cx,
+    w_i2h_words,
+    w_i2h_scales,
+    b_i2h,
+    w_h2h_words,
+    w_h2h_scales,
+    b_h2h,
+    ln_i2h_w,
+    ln_i2h_b,
+    ln_h2h_w,
+    ln_h2h_b,
+    ln_h2o_w,
+    ln_h2o_b,
+    out_0,
+    out_1,
+):
+    nc = tc.nc
+    with ExitStack() as stack:
+        keep = stack.enter_context(tc.tile_pool(name="keep", bufs=1))
+        small = stack.enter_context(tc.tile_pool(name="small", bufs=1))
+        stage = stack.enter_context(tc.tile_pool(name="stage", bufs=2))
+        weights = stack.enter_context(tc.tile_pool(name="weights", bufs=8))
+        sums = stack.enter_context(tc.psum_pool(name="sums", bufs=1))
+        banks = stack.enter_context(tc.psum_pool(name="banks", bufs=4))
+
+        half = small.tile([P, 1], F32, name="half")
+        nc.vector.memset(half[:], 0.5)
+        forget_bias = small.tile([P, 1], F32, name="forget_bias")
+        nc.vector.memset(forget_bias[:], FORGET_GATE_BIAS)
+        warm = small.tile([P, 1], F32, name="warm")
+        nc.scalar.activation(out=warm[:], in_=forget_bias[:], func=ACT.Sigmoid)
+
+        rows = keep.tile([P, WIDE], BF16, name="rows")
+        nc.vector.memset(rows[:], 0.0)
+        w_planes = keep.tile([P, GROUPS // PLANES + 1, WIDE], U8, name="w_planes", align_bytes=64)
+        nc.vector.memset(w_planes[:].rearrange("p c n -> p (c n)").bitcast(I32), 0)
+
+        ident_f32 = keep.tile([P, P], F32, name="ident_f32")
+        make_identity(nc, ident_f32[:])
+        ident_bf16 = keep.tile([P, P], BF16, name="ident_bf16")
+        make_identity(nc, ident_bf16[:])
+
+        x_sb = keep.tile([P, IN], BF16, name="x_sb")
+        chunk_cols = CHUNK * K_PASS
+        for c in range(X_GROUPS // CHUNK):
+            cols = slice(c * chunk_cols, (c + 1) * chunk_cols)
+            nc.sync.dma_start(out=x_sb[:, cols], in_=inputs[:, cols])
+        hx_sb = keep.tile([P, HID], BF16, name="hx_sb")
+        nc.sync.dma_start(out=hx_sb[:], in_=hx[:, :])
+
+        nc.scalar.dma_start(out=rows[ROW_B_H2H : ROW_B_H2H + 1, :], in_=b_h2h.rearrange("(o n) -> o n", o=1))
+        nc.scalar.dma_start(out=rows[ROW_W_H2H : ROW_W_H2H + 1, :], in_=ln_h2h_w[:, :])
+        nc.scalar.dma_start(out=rows[ROW_S_H2H : ROW_S_H2H + 1, :], in_=ln_h2h_b[:, :])
+        nc.scalar.dma_start(out=rows[ROW_S_I2H : ROW_S_I2H + 1, :], in_=ln_i2h_b[:, :])
+        nc.scalar.dma_start(out=rows[ROW_B_I2H : ROW_B_I2H + 1, :], in_=b_i2h.rearrange("(o n) -> o n", o=1))
+        nc.scalar.dma_start(out=rows[ROW_W_I2H : ROW_W_I2H + 1, :], in_=ln_i2h_w[:, :])
+        nc.scalar.dma_start(out=rows[ROW_H2O : ROW_H2O + 1, 0:HID], in_=ln_h2o_w[:, :])
+        nc.scalar.dma_start(out=rows[ROW_H2O : ROW_H2O + 1, HID : 2 * HID], in_=ln_h2o_b[:, :])
+        cx_sb = keep.tile([P, HID], BF16, name="cx_sb")
+        nc.scalar.dma_start(out=cx_sb[:], in_=cx[:, :])
+
+        planes_i32 = w_planes[:].bitcast(I32)
+        for c in range(X_GROUPS // PLANES):
+            for quad in range(4):
+                nc.sync.dma_start(
+                    out=planes_i32[32 * quad : 32 * quad + 4 * PLANES, c, :],
+                    in_=w_i2h_scales[PLANES * c : PLANES * (c + 1), 4 * quad : 4 * quad + 4, :].bitcast(I32),
+                )
+        for quad in range(4):
+            nc.sync.dma_start(
+                out=planes_i32[32 * quad : 32 * quad + 4, H_GROUP // PLANES, :],
+                in_=w_h2h_scales[0, 4 * quad : 4 * quad + 4, :].bitcast(I32),
+            )
+
+        def weight_plane(g, cols):
+            first = 4 * (g % PLANES)
+            return w_planes[first:P, g // PLANES, cols]
+
+        x_codes = keep.tile([P, GROUPS, P], U32, name="x_codes", align_bytes=64)
+        x_planes = keep.tile([P, GROUPS, P], U8, name="x_planes", align_bytes=64)
+
+        def transpose_pair(source_words, first_group, n_groups, grouped, engine_copy):
+            flipped = banks.tile([P, n_groups, 2, P], F32, name="flipped", tag="bank")
+            for i in range(n_groups):
+                base = (first_group + i) * (K_PASS // 2)
+                for u in range(2):
+                    nc.tensor.transpose(
+                        flipped[:, i, u, :],
+                        source_words[:, base + u : base + K_PASS // 2 : 2],
+                        ident_f32[:],
+                    )
+            engine_copy(out=grouped.bitcast(F32), in_=flipped[:].rearrange("p g u r -> p g r u"))
+
+        x_words = x_sb[:].bitcast(F32)
+        for c in range(X_GROUPS // CHUNK):
+            grouped = stage.tile([P, CHUNK, P, PACK], BF16, name="grouped", align_bytes=64)
+            transpose_pair(x_words, CHUNK * c, 2, grouped[:, 0:2, :, :], nc.vector.tensor_copy)
+            transpose_pair(x_words, CHUNK * c + 2, 2, grouped[:, 2:4, :, :], nc.scalar.copy)
+            groups = slice(CHUNK * c, CHUNK * (c + 1))
+            nc.vector.quantize_mx(
+                out=x_codes[:, groups, :].rearrange("p g r -> p (g r)").bitcast(FP8X4),
+                scales=x_planes[:, groups, :].rearrange("p g r -> p (g r)"),
+                in_=grouped[:].rearrange("p g r t -> p (g r t)"),
+            )
+        grouped_h = stage.tile([P, 1, P, PACK], BF16, name="grouped_h", align_bytes=64)
+        transpose_pair(hx_sb[:].bitcast(F32), 0, 1, grouped_h[:], nc.vector.tensor_copy)
+        nc.vector.quantize_mx(
+            out=x_codes[:, H_GROUP, :].bitcast(FP8X4),
+            scales=x_planes[:, H_GROUP, :],
+            in_=grouped_h[:].rearrange("p g r t -> p (g r t)"),
+        )
+
+        def mx_pass(acc, g, w_words, cols, start, stop):
+            nc.tensor.matmul_mx(
+                out=acc,
+                lhsT=x_codes[:, g, :].bitcast(FP8X4),
+                lhsT_scale=x_planes[:, g, :],
+                rhs=w_words.bitcast(FP8X4),
+                rhs_scale=weight_plane(g, cols),
+                start=start,
+                stop=stop,
+            )
+
+        both_shifts = small.tile([P, 1], BF16, name="both_shifts")
+        nc.vector.tensor_add(
+            out=both_shifts[:],
+            in0=ident_bf16[:, ROW_S_I2H : ROW_S_I2H + 1],
+            in1=ident_bf16[:, ROW_S_H2H : ROW_S_H2H + 1],
+        )
+
+        def spread(pick, width, label):
+            wide = keep.tile([P, width], F32, name=label)
+            for first in range(0, width, HID):
+                cols = slice(first, first + HID)
+                bank = banks.tile([P, HID], F32, name="bank", tag="bank")
+                nc.tensor.matmul(
+                    bank[:], lhsT=pick.to_broadcast([P, P]), rhs=rows[:, cols], start=True, stop=True
+                )
+                nc.scalar.copy(out=wide[:, cols], in_=bank[:])
+            return wide
+
+        bias_h2h = spread(ident_bf16[:, ROW_B_H2H : ROW_B_H2H + 1], WIDE, "bias_h2h")
+        gain_h2h = spread(ident_bf16[:, ROW_W_H2H : ROW_W_H2H + 1], WIDE, "gain_h2h")
+        shift = spread(both_shifts[:], WIDE, "shift")
+        bias_i2h = spread(ident_bf16[:, ROW_B_I2H : ROW_B_I2H + 1], WIDE, "bias_i2h")
+        gain_i2h = spread(ident_bf16[:, ROW_W_I2H : ROW_W_I2H + 1], WIDE, "gain_i2h")
+        h2o = spread(ident_bf16[:, ROW_H2O : ROW_H2O + 1], 2 * HID, "h2o")
+        gain_h2o = h2o[:, 0:HID]
+        shift_h2o = h2o[:, HID : 2 * HID]
+
+        gate_cols = [slice(j * HID, (j + 1) * HID) for j in range(GATES)]
+
+        w_h = weights.tile([P, WIDE], U32, name="w_h", tag="w", align_bytes=64)
+        nc.sync.dma_start(
+            out=w_h[:].bitcast(I32), in_=w_h2h_words[0].rearrange("p n t -> p (n t)").bitcast(I32)
+        )
+        h2h = keep.tile([P, WIDE], F32, name="h2h")
+        stats_h2h = small.tile([P, GATES, 6], F32, name="stats_h2h")
+        for j in range(GATES):
+            bank = banks.tile([P, HID], F32, name="bank", tag="bank")
+            mx_pass(bank[:], H_GROUP, w_h[:, gate_cols[j]], gate_cols[j], True, True)
+            nc.vector.tensor_add(out=h2h[:, gate_cols[j]], in0=bank[:], in1=bias_h2h[:, gate_cols[j]])
+            nc.vector.bn_stats(out=stats_h2h[:, j, :], in_=h2h[:, gate_cols[j]])
+        mean_h, rstd_h = mean_and_rstd(
+            nc, small, stats_h2h[:].rearrange("p c s -> p (c s)"), WIDE, half, "h2h"
+        )
+        for j in range(GATES):
+            cols = gate_cols[j]
+            centre_times_gain(nc, h2h[:, cols], h2h[:, cols], mean_h, gain_h2h[:, cols])
+            scale_plus_shift(nc, shift[:, cols], h2h[:, cols], rstd_h, shift[:, cols])
+
+        acc = [sums.tile([P, HID], F32, name="acc%d" % j) for j in range(GATES)]
+        for g in range(MAIN):
+            w_g = weights.tile([P, WIDE], U32, name="w_g", tag="w", align_bytes=64)
+            nc.sync.dma_start(
+                out=w_g[:].bitcast(I32), in_=w_i2h_words[g].rearrange("p n t -> p (n t)").bitcast(I32)
+            )
+            for j in range(GATES):
+                mx_pass(acc[j][:], g, w_g[:, gate_cols[j]], gate_cols[j], g == 0, False)
+        i2h = keep.tile([P, WIDE], F32, name="i2h")
+        stats_i2h = small.tile([P, GATES, 6], F32, name="stats_i2h")
+        for j in range(GATES):
+            cols = gate_cols[j]
+            w_j = weights.tile([P, LAST, HID], U32, name="w_j", tag="w", align_bytes=64)
+            nc.sync.dma_start(
+                out=w_j[:].bitcast(I32),
+                in_=w_i2h_words[MAIN:X_GROUPS, :, cols, :].rearrange("g p n t -> p g (n t)").bitcast(I32),
+            )
+            for i in range(LAST):
+                mx_pass(acc[j][:], MAIN + i, w_j[:, i, :], cols, False, i == LAST - 1)
+            nc.vector.tensor_add(out=i2h[:, cols], in0=acc[j][:], in1=bias_i2h[:, cols])
+            nc.vector.bn_stats(out=stats_i2h[:, j, :], in_=i2h[:, cols])
+        mean_i, rstd_i = mean_and_rstd(
+            nc, small, stats_i2h[:].rearrange("p c s -> p (c s)"), WIDE, half, "i2h"
+        )
+
+        gate = keep.tile([P, WIDE], F32, name="gate")
+
+        def make_gate(j, func, bias):
+            cols = gate_cols[j]
+            centre_times_gain(nc, gate[:, cols], i2h[:, cols], mean_i, gain_i2h[:, cols])
+            scale_plus_shift(nc, gate[:, cols], gate[:, cols], rstd_i, shift[:, cols])
+            if bias is None:
+                nc.scalar.activation(out=gate[:, cols], in_=gate[:, cols], func=func)
+            else:
+                nc.scalar.activation(out=gate[:, cols], in_=gate[:, cols], func=func, bias=bias)
+
+        make_gate(GATE_F, ACT.Sigmoid, forget_bias[:])
+        make_gate(GATE_I, ACT.Sigmoid, None)
+        make_gate(GATE_C, ACT.Tanh, None)
+
+        kept = keep.tile([P, HID], F32, name="kept")
+        nc.vector.tensor_mul(out=kept[:], in0=gate[:, gate_cols[GATE_F]], in1=cx_sb[:])
+        fresh = keep.tile([P, HID], F32, name="fresh")
+        nc.vector.tensor_mul(out=fresh[:], in0=gate[:, gate_cols[GATE_I]], in1=gate[:, gate_cols[GATE_C]])
+        cx_new = keep.tile([P, HID], F32, name="cx_new")
+        nc.vector.tensor_add(out=cx_new[:], in0=kept[:], in1=fresh[:])
+        nc.sync.dma_start(out=out_1[:, :], in_=cx_new[:])
+
+        stats_c = small.tile([P, 6], F32, name="stats_c")
+        nc.vector.bn_stats(out=stats_c[:], in_=cx_new[:])
+        mean_c, rstd_c = mean_and_rstd(nc, small, stats_c[:], HID, half, "h2o")
+        make_gate(GATE_O, ACT.Sigmoid, None)
+
+        cell = keep.tile([P, HID], F32, name="cell")
+        centre_times_gain(nc, cell[:], cx_new[:], mean_c, gain_h2o)
+        scale_plus_shift(nc, cell[:], cell[:], rstd_c, shift_h2o)
+        nc.scalar.activation(out=cell[:], in_=cell[:], func=ACT.Tanh)
+        hx_new = keep.tile([P, HID], F32, name="hx_new")
+        nc.vector.tensor_mul(out=hx_new[:], in0=gate[:, gate_cols[GATE_O]], in1=cell[:])
+        nc.sync.dma_start(out=out_0[:, :], in_=hx_new[:])

@@ -33,6 +33,7 @@ GROUPS = X_GROUPS + 1
 CHUNK = 4
 PLANES = 4
 LAST = 4
+PIECE = 2
 MAIN = X_GROUPS - LAST
 
 ROW_B_I2H = 0
@@ -46,23 +47,31 @@ ROW_H2O = 6
 FLOPS = 2 * P * (IN + HID) * WIDE
 
 
-def mean_and_rstd(nc, small, stats, count, half, label):
+def mean_and_root(nc, small, stats, half, label):
     mean_var = small.tile([P, 2], F32, name="mean_var_" + label)
     nc.vector.bn_aggr(out=mean_var[:], in_=stats)
     root = small.tile([P, 1], F32, name="root_" + label)
     nc.gpsimd.tensor_tensor(out=root[:], in0=mean_var[:, 1:2], in1=half[:], op=ALU.pow)
+    return mean_var[:, 0:1], root[:]
+
+
+def unbiased_std_plus_eps(nc, small, root, count, label):
     std_eps = small.tile([P, 1], F32, name="std_eps_" + label)
     nc.vector.tensor_scalar(
         out=std_eps[:],
-        in0=root[:],
+        in0=root,
         scalar1=math.sqrt(count / (count - 1.0)),
         scalar2=EPS,
         op0=ALU.mult,
         op1=ALU.add,
     )
-    rstd = small.tile([P, 1], F32, name="rstd_" + label)
-    nc.vector.reciprocal(out=rstd[:], in_=std_eps[:])
-    return mean_var[:, 0:1], rstd[:]
+    return std_eps[:]
+
+
+def one_over(nc, small, value, label):
+    inverse = small.tile([P, 1], F32, name="inverse_" + label)
+    nc.vector.reciprocal(out=inverse[:], in_=value)
+    return inverse[:]
 
 
 def centre_times_gain(nc, out, value, mean, gain):
@@ -71,9 +80,9 @@ def centre_times_gain(nc, out, value, mean, gain):
     )
 
 
-def scale_plus_shift(nc, out, value, rstd, shift):
+def times_scalar_plus(nc, out, value, scalar, other):
     nc.vector.scalar_tensor_tensor(
-        out=out, in0=value, scalar=rstd, in1=shift, op0=ALU.mult, op1=ALU.add
+        out=out, in0=value, scalar=scalar, in1=other, op0=ALU.mult, op1=ALU.add
     )
 
 
@@ -244,13 +253,12 @@ def tile_layernormlstmcell_k_kernel(
             mx_pass(bank[:], H_GROUP, w_h[:, gate_cols[j]], gate_cols[j], True, True)
             nc.vector.tensor_add(out=h2h[:, gate_cols[j]], in0=bank[:], in1=bias_h2h[:, gate_cols[j]])
             nc.vector.bn_stats(out=stats_h2h[:, j, :], in_=h2h[:, gate_cols[j]])
-        mean_h, rstd_h = mean_and_rstd(
-            nc, small, stats_h2h[:].rearrange("p c s -> p (c s)"), WIDE, half, "h2h"
-        )
+        mean_h, root_h = mean_and_root(nc, small, stats_h2h[:].rearrange("p c s -> p (c s)"), half, "h2h")
+        rstd_h = one_over(nc, small, unbiased_std_plus_eps(nc, small, root_h, WIDE, "h2h"), "h2h")
         for j in range(GATES):
             cols = gate_cols[j]
             centre_times_gain(nc, h2h[:, cols], h2h[:, cols], mean_h, gain_h2h[:, cols])
-            scale_plus_shift(nc, shift[:, cols], h2h[:, cols], rstd_h, shift[:, cols])
+            times_scalar_plus(nc, shift[:, cols], h2h[:, cols], rstd_h, shift[:, cols])
 
         acc = [sums.tile([P, HID], F32, name="acc%d" % j) for j in range(GATES)]
         for g in range(MAIN):
@@ -260,55 +268,72 @@ def tile_layernormlstmcell_k_kernel(
             )
             for j in range(GATES):
                 mx_pass(acc[j][:], g, w_g[:, gate_cols[j]], gate_cols[j], g == 0, False)
+        stack.enter_context(tc.manual_schedule())
+
         i2h = keep.tile([P, WIDE], F32, name="i2h")
         stats_i2h = small.tile([P, GATES, 6], F32, name="stats_i2h")
         for j in range(GATES):
             cols = gate_cols[j]
-            w_j = weights.tile([P, LAST, HID], U32, name="w_j", tag="w", align_bytes=64)
-            nc.sync.dma_start(
-                out=w_j[:].bitcast(I32),
-                in_=w_i2h_words[MAIN:X_GROUPS, :, cols, :].rearrange("g p n t -> p g (n t)").bitcast(I32),
-            )
-            for i in range(LAST):
-                mx_pass(acc[j][:], MAIN + i, w_j[:, i, :], cols, False, i == LAST - 1)
+            for first in range(MAIN, X_GROUPS, PIECE):
+                w_j = weights.tile([P, PIECE, HID], U32, name="w_j", tag="w", align_bytes=64)
+                nc.sync.dma_start(
+                    out=w_j[:].bitcast(I32),
+                    in_=w_i2h_words[first : first + PIECE, :, cols, :]
+                    .rearrange("g p n t -> p g (n t)")
+                    .bitcast(I32),
+                )
+                for i in range(PIECE):
+                    mx_pass(acc[j][:], first + i, w_j[:, i, :], cols, False, first + i == X_GROUPS - 1)
             nc.vector.tensor_add(out=i2h[:, cols], in0=acc[j][:], in1=bias_i2h[:, cols])
             nc.vector.bn_stats(out=stats_i2h[:, j, :], in_=i2h[:, cols])
-        mean_i, rstd_i = mean_and_rstd(
-            nc, small, stats_i2h[:].rearrange("p c s -> p (c s)"), WIDE, half, "i2h"
-        )
 
         gate = keep.tile([P, WIDE], F32, name="gate")
 
-        def make_gate(j, func, bias):
+        def gate_centre(j):
             cols = gate_cols[j]
             centre_times_gain(nc, gate[:, cols], i2h[:, cols], mean_i, gain_i2h[:, cols])
-            scale_plus_shift(nc, gate[:, cols], gate[:, cols], rstd_i, shift[:, cols])
-            if bias is None:
-                nc.scalar.activation(out=gate[:, cols], in_=gate[:, cols], func=func)
-            else:
-                nc.scalar.activation(out=gate[:, cols], in_=gate[:, cols], func=func, bias=bias)
 
-        make_gate(GATE_F, ACT.Sigmoid, forget_bias[:])
-        make_gate(GATE_I, ACT.Sigmoid, None)
-        make_gate(GATE_C, ACT.Tanh, None)
+        def gate_add_shift(j):
+            cols = gate_cols[j]
+            times_scalar_plus(nc, gate[:, cols], shift[:, cols], std_i, gate[:, cols])
+
+        mean_i, root_i = mean_and_root(nc, small, stats_i2h[:].rearrange("p c s -> p (c s)"), half, "i2h")
+        gate_centre(GATE_F)
+        gate_centre(GATE_I)
+        gate_centre(GATE_C)
+        std_i = unbiased_std_plus_eps(nc, small, root_i, WIDE, "i2h")
+        gate_add_shift(GATE_F)
+        rstd_i = one_over(nc, small, std_i, "i2h")
+        gate_add_shift(GATE_I)
+        gate_add_shift(GATE_C)
+        forget = gate[:, gate_cols[GATE_F]]
+        nc.scalar.activation(out=forget, in_=forget, func=ACT.Sigmoid, scale=rstd_i, bias=forget_bias[:])
+        take_in = gate[:, gate_cols[GATE_I]]
+        nc.scalar.activation(out=take_in, in_=take_in, func=ACT.Sigmoid, scale=rstd_i)
+        candidate = gate[:, gate_cols[GATE_C]]
+        nc.scalar.activation(out=candidate, in_=candidate, func=ACT.Tanh, scale=rstd_i)
 
         kept = keep.tile([P, HID], F32, name="kept")
-        nc.vector.tensor_mul(out=kept[:], in0=gate[:, gate_cols[GATE_F]], in1=cx_sb[:])
+        nc.vector.tensor_mul(out=kept[:], in0=forget, in1=cx_sb[:])
+        gate_centre(GATE_O)
         fresh = keep.tile([P, HID], F32, name="fresh")
-        nc.vector.tensor_mul(out=fresh[:], in0=gate[:, gate_cols[GATE_I]], in1=gate[:, gate_cols[GATE_C]])
+        nc.vector.tensor_mul(out=fresh[:], in0=take_in, in1=candidate)
         cx_new = keep.tile([P, HID], F32, name="cx_new")
         nc.vector.tensor_add(out=cx_new[:], in0=kept[:], in1=fresh[:])
         nc.sync.dma_start(out=out_1[:, :], in_=cx_new[:])
 
         stats_c = small.tile([P, 6], F32, name="stats_c")
         nc.vector.bn_stats(out=stats_c[:], in_=cx_new[:])
-        mean_c, rstd_c = mean_and_rstd(nc, small, stats_c[:], HID, half, "h2o")
-        make_gate(GATE_O, ACT.Sigmoid, None)
-
+        mean_c, root_c = mean_and_root(nc, small, stats_c[:], half, "h2o")
         cell = keep.tile([P, HID], F32, name="cell")
         centre_times_gain(nc, cell[:], cx_new[:], mean_c, gain_h2o)
-        scale_plus_shift(nc, cell[:], cell[:], rstd_c, shift_h2o)
-        nc.scalar.activation(out=cell[:], in_=cell[:], func=ACT.Tanh)
+        gate_add_shift(GATE_O)
+        let_out = gate[:, gate_cols[GATE_O]]
+        nc.scalar.activation(out=let_out, in_=let_out, func=ACT.Sigmoid, scale=rstd_i)
+        std_c = unbiased_std_plus_eps(nc, small, root_c, HID, "h2o")
+        times_scalar_plus(nc, cell[:], shift_h2o, std_c, cell[:])
+        rstd_c = one_over(nc, small, std_c, "h2o")
+        nc.scalar.activation(out=cell[:], in_=cell[:], func=ACT.Tanh, scale=rstd_c)
         hx_new = keep.tile([P, HID], F32, name="hx_new")
-        nc.vector.tensor_mul(out=hx_new[:], in0=gate[:, gate_cols[GATE_O]], in1=cell[:])
+        nc.vector.tensor_mul(out=hx_new[:], in0=let_out, in1=cell[:])
         nc.sync.dma_start(out=out_0[:, :], in_=hx_new[:])

@@ -115,6 +115,8 @@ def tile_layernormlstmcell_k_kernel(
         sums = stack.enter_context(tc.psum_pool(name="sums", bufs=1))
         banks = stack.enter_context(tc.psum_pool(name="banks", bufs=4))
 
+        w_planes = keep.tile([P, GROUPS // PLANES + 1, WIDE], U8, name="w_planes", align_bytes=64)
+        nc.vector.memset(w_planes[:].rearrange("p c n -> p (c n)").bitcast(I32), 0)
         half = small.tile([P, 1], F32, name="half")
         nc.vector.memset(half[:], 0.5)
         forget_bias = small.tile([P, 1], F32, name="forget_bias")
@@ -124,8 +126,6 @@ def tile_layernormlstmcell_k_kernel(
 
         rows = keep.tile([P, WIDE], BF16, name="rows")
         nc.vector.memset(rows[:], 0.0)
-        w_planes = keep.tile([P, GROUPS // PLANES + 1, WIDE], U8, name="w_planes", align_bytes=64)
-        nc.vector.memset(w_planes[:].rearrange("p c n -> p (c n)").bitcast(I32), 0)
 
         ident_f32 = keep.tile([P, P], F32, name="ident_f32")
         make_identity(nc, ident_f32[:])
@@ -151,18 +151,23 @@ def tile_layernormlstmcell_k_kernel(
         cx_sb = keep.tile([P, HID], BF16, name="cx_sb")
         nc.scalar.dma_start(out=cx_sb[:], in_=cx[:, :])
 
-        planes_i32 = w_planes[:].bitcast(I32)
-        for c in range(X_GROUPS // PLANES):
+        planes_f32 = w_planes[:].bitcast(F32)
+
+        def load_planes(c):
             for quad in range(4):
-                nc.sync.dma_start(
-                    out=planes_i32[32 * quad : 32 * quad + 4 * PLANES, c, :],
-                    in_=w_i2h_scales[PLANES * c : PLANES * (c + 1), 4 * quad : 4 * quad + 4, :].bitcast(I32),
+                nc.gpsimd.dma_start(
+                    out=planes_f32[32 * quad : 32 * quad + 4 * PLANES, c, :],
+                    in_=w_i2h_scales[PLANES * c : PLANES * (c + 1), 4 * quad : 4 * quad + 4, :].bitcast(F32),
                 )
+
+        load_planes(0)
         for quad in range(4):
-            nc.sync.dma_start(
-                out=planes_i32[32 * quad : 32 * quad + 4, H_GROUP // PLANES, :],
-                in_=w_h2h_scales[0, 4 * quad : 4 * quad + 4, :].bitcast(I32),
+            nc.gpsimd.dma_start(
+                out=planes_f32[32 * quad : 32 * quad + 4, H_GROUP // PLANES, :],
+                in_=w_h2h_scales[0, 4 * quad : 4 * quad + 4, :].bitcast(F32),
             )
+        for c in range(1, X_GROUPS // PLANES):
+            load_planes(c)
 
         def weight_plane(g, cols):
             first = 4 * (g % PLANES)

@@ -34,6 +34,7 @@ CHUNK = 4
 PLANES = 4
 LAST = 4
 PIECE = 2
+HALF = HID // 2
 MAIN = X_GROUPS - LAST
 
 ROW_B_I2H = 0
@@ -154,7 +155,7 @@ def tile_layernormlstmcell_k_kernel(
         planes_f32 = w_planes[:].bitcast(F32)
 
         def load_planes(c):
-            for quad in range(4):
+            for quad in (0, 2, 1, 3):
                 nc.gpsimd.dma_start(
                     out=planes_f32[32 * quad : 32 * quad + 4 * PLANES, c, :],
                     in_=w_i2h_scales[PLANES * c : PLANES * (c + 1), 4 * quad : 4 * quad + 4, :].bitcast(F32),
@@ -276,7 +277,8 @@ def tile_layernormlstmcell_k_kernel(
         stack.enter_context(tc.manual_schedule())
 
         i2h = keep.tile([P, WIDE], F32, name="i2h")
-        stats_i2h = small.tile([P, GATES, 6], F32, name="stats_i2h")
+        stats_i2h = small.tile([P, GATES, 2, 6], F32, name="stats_i2h")
+        halves = [slice(0, HALF), slice(HALF, HID)]
         for j in range(GATES):
             cols = gate_cols[j]
             for first in range(MAIN, X_GROUPS, PIECE):
@@ -289,8 +291,12 @@ def tile_layernormlstmcell_k_kernel(
                 )
                 for i in range(PIECE):
                     mx_pass(acc[j][:], first + i, w_j[:, i, :], cols, False, first + i == X_GROUPS - 1)
-            nc.vector.tensor_add(out=i2h[:, cols], in0=acc[j][:], in1=bias_i2h[:, cols])
-            nc.vector.bn_stats(out=stats_i2h[:, j, :], in_=i2h[:, cols])
+            for part in halves:
+                nc.vector.tensor_add(
+                    out=i2h[:, cols][:, part], in0=acc[j][:, part], in1=bias_i2h[:, cols][:, part]
+                )
+            for h in range(2):
+                nc.vector.bn_stats(out=stats_i2h[:, j, h, :], in_=i2h[:, cols][:, halves[h]])
 
         gate = keep.tile([P, WIDE], F32, name="gate")
 
@@ -302,7 +308,7 @@ def tile_layernormlstmcell_k_kernel(
             cols = gate_cols[j]
             times_scalar_plus(nc, gate[:, cols], shift[:, cols], std_i, gate[:, cols])
 
-        mean_i, root_i = mean_and_root(nc, small, stats_i2h[:].rearrange("p c s -> p (c s)"), half, "i2h")
+        mean_i, root_i = mean_and_root(nc, small, stats_i2h[:].rearrange("p c h s -> p (c h s)"), half, "i2h")
         gate_centre(GATE_F)
         gate_centre(GATE_I)
         gate_centre(GATE_C)
@@ -322,23 +328,29 @@ def tile_layernormlstmcell_k_kernel(
         nc.vector.tensor_mul(out=kept[:], in0=forget, in1=cx_sb[:])
         gate_centre(GATE_O)
         fresh = keep.tile([P, HID], F32, name="fresh")
-        nc.vector.tensor_mul(out=fresh[:], in0=take_in, in1=candidate)
+        for part in halves:
+            nc.vector.tensor_mul(out=fresh[:, part], in0=take_in[:, part], in1=candidate[:, part])
         cx_new = keep.tile([P, HID], F32, name="cx_new")
-        nc.vector.tensor_add(out=cx_new[:], in0=kept[:], in1=fresh[:])
+        for part in halves:
+            nc.vector.tensor_add(out=cx_new[:, part], in0=kept[:, part], in1=fresh[:, part])
+        stats_c = small.tile([P, 2, 6], F32, name="stats_c")
+        for h in range(2):
+            nc.vector.bn_stats(out=stats_c[:, h, :], in_=cx_new[:, halves[h]])
         nc.sync.dma_start(out=out_1[:, :], in_=cx_new[:])
 
-        stats_c = small.tile([P, 6], F32, name="stats_c")
-        nc.vector.bn_stats(out=stats_c[:], in_=cx_new[:])
-        mean_c, root_c = mean_and_root(nc, small, stats_c[:], half, "h2o")
+        mean_c, root_c = mean_and_root(nc, small, stats_c[:].rearrange("p h s -> p (h s)"), half, "h2o")
         cell = keep.tile([P, HID], F32, name="cell")
         centre_times_gain(nc, cell[:], cx_new[:], mean_c, gain_h2o)
         gate_add_shift(GATE_O)
         let_out = gate[:, gate_cols[GATE_O]]
         nc.scalar.activation(out=let_out, in_=let_out, func=ACT.Sigmoid, scale=rstd_i)
         std_c = unbiased_std_plus_eps(nc, small, root_c, HID, "h2o")
-        times_scalar_plus(nc, cell[:], shift_h2o, std_c, cell[:])
+        times_scalar_plus(nc, cell[:, halves[0]], shift_h2o[:, halves[0]], std_c, cell[:, halves[0]])
         rstd_c = one_over(nc, small, std_c, "h2o")
-        nc.scalar.activation(out=cell[:], in_=cell[:], func=ACT.Tanh, scale=rstd_c)
+        times_scalar_plus(nc, cell[:, halves[1]], shift_h2o[:, halves[1]], std_c, cell[:, halves[1]])
         hx_new = keep.tile([P, HID], F32, name="hx_new")
-        nc.vector.tensor_mul(out=hx_new[:], in0=let_out, in1=cell[:])
-        nc.sync.dma_start(out=out_0[:, :], in_=hx_new[:])
+        for part in halves:
+            nc.scalar.activation(out=cell[:, part], in_=cell[:, part], func=ACT.Tanh, scale=rstd_c)
+        for part in halves:
+            nc.vector.tensor_mul(out=hx_new[:, part], in0=let_out[:, part], in1=cell[:, part])
+            nc.sync.dma_start(out=out_0[:, part], in_=hx_new[:, part])

@@ -113,11 +113,9 @@ def tile_layernormlstmcell_k_kernel(
         small = stack.enter_context(tc.tile_pool(name="small", bufs=1))
         stage = stack.enter_context(tc.tile_pool(name="stage", bufs=2))
         weights = stack.enter_context(tc.tile_pool(name="weights", bufs=8))
-        sums = stack.enter_context(tc.psum_pool(name="sums", bufs=1))
-        banks = stack.enter_context(tc.psum_pool(name="banks", bufs=4))
+        banks = stack.enter_context(tc.psum_pool(name="banks", bufs=1))
+        stack.enter_context(tc.manual_schedule())
 
-        w_planes = keep.tile([P, GROUPS // PLANES + 1, WIDE], U8, name="w_planes", align_bytes=64)
-        nc.vector.memset(w_planes[:].rearrange("p c n -> p (c n)").bitcast(I32), 0)
         half = small.tile([P, 1], F32, name="half")
         nc.vector.memset(half[:], 0.5)
         forget_bias = small.tile([P, 1], F32, name="forget_bias")
@@ -125,13 +123,27 @@ def tile_layernormlstmcell_k_kernel(
         warm = small.tile([P, 1], F32, name="warm")
         nc.scalar.activation(out=warm[:], in_=forget_bias[:], func=ACT.Sigmoid)
 
+        w_planes = keep.tile([P, GROUPS // PLANES + 1, WIDE], U8, name="w_planes", align_bytes=64)
         rows = keep.tile([P, WIDE], BF16, name="rows")
-        nc.vector.memset(rows[:], 0.0)
+
+        def zero_planes(c):
+            nc.vector.memset(w_planes[:, c, :].bitcast(I32), 0)
+
+        zero_planes(H_GROUP // PLANES)
+        nc.vector.memset(rows[:].bitcast(I32), 0)
+        for c in range(X_GROUPS // PLANES):
+            zero_planes(c)
 
         ident_f32 = keep.tile([P, P], F32, name="ident_f32")
         make_identity(nc, ident_f32[:])
         ident_bf16 = keep.tile([P, P], BF16, name="ident_bf16")
         make_identity(nc, ident_bf16[:])
+        both_shifts = small.tile([P, 1], BF16, name="both_shifts")
+        nc.vector.tensor_add(
+            out=both_shifts[:],
+            in0=ident_bf16[:, ROW_S_I2H : ROW_S_I2H + 1],
+            in1=ident_bf16[:, ROW_S_H2H : ROW_S_H2H + 1],
+        )
 
         x_sb = keep.tile([P, IN], BF16, name="x_sb")
         chunk_cols = CHUNK * K_PASS
@@ -141,34 +153,27 @@ def tile_layernormlstmcell_k_kernel(
         hx_sb = keep.tile([P, HID], BF16, name="hx_sb")
         nc.sync.dma_start(out=hx_sb[:], in_=hx[:, :])
 
-        nc.scalar.dma_start(out=rows[ROW_B_H2H : ROW_B_H2H + 1, :], in_=b_h2h.rearrange("(o n) -> o n", o=1))
-        nc.scalar.dma_start(out=rows[ROW_W_H2H : ROW_W_H2H + 1, :], in_=ln_h2h_w[:, :])
-        nc.scalar.dma_start(out=rows[ROW_S_H2H : ROW_S_H2H + 1, :], in_=ln_h2h_b[:, :])
-        nc.scalar.dma_start(out=rows[ROW_S_I2H : ROW_S_I2H + 1, :], in_=ln_i2h_b[:, :])
-        nc.scalar.dma_start(out=rows[ROW_B_I2H : ROW_B_I2H + 1, :], in_=b_i2h.rearrange("(o n) -> o n", o=1))
-        nc.scalar.dma_start(out=rows[ROW_W_I2H : ROW_W_I2H + 1, :], in_=ln_i2h_w[:, :])
-        nc.scalar.dma_start(out=rows[ROW_H2O : ROW_H2O + 1, 0:HID], in_=ln_h2o_w[:, :])
-        nc.scalar.dma_start(out=rows[ROW_H2O : ROW_H2O + 1, HID : 2 * HID], in_=ln_h2o_b[:, :])
-        cx_sb = keep.tile([P, HID], BF16, name="cx_sb")
-        nc.scalar.dma_start(out=cx_sb[:], in_=cx[:, :])
+        def load_row(row, source, first=0):
+            width = source.shape[1]
+            nc.scalar.dma_start(out=rows[row : row + 1, first : first + width], in_=source)
+
+        load_row(ROW_B_H2H, b_h2h.rearrange("(o n) -> o n", o=1))
+        load_row(ROW_W_H2H, ln_h2h_w)
+        load_row(ROW_S_H2H, ln_h2h_b)
+        load_row(ROW_S_I2H, ln_i2h_b)
 
         planes_f32 = w_planes[:].bitcast(F32)
-
-        def load_planes(c):
-            for quad in (0, 2, 1, 3):
-                nc.gpsimd.dma_start(
-                    out=planes_f32[32 * quad : 32 * quad + 4 * PLANES, c, :],
-                    in_=w_i2h_scales[PLANES * c : PLANES * (c + 1), 4 * quad : 4 * quad + 4, :].bitcast(F32),
-                )
-
-        load_planes(0)
         for quad in range(4):
             nc.gpsimd.dma_start(
                 out=planes_f32[32 * quad : 32 * quad + 4, H_GROUP // PLANES, :],
                 in_=w_h2h_scales[0, 4 * quad : 4 * quad + 4, :].bitcast(F32),
             )
-        for c in range(1, X_GROUPS // PLANES):
-            load_planes(c)
+        for c in range(X_GROUPS // PLANES):
+            for quad in (0, 2, 1, 3):
+                nc.gpsimd.dma_start(
+                    out=planes_f32[32 * quad : 32 * quad + 4 * PLANES, c, :],
+                    in_=w_i2h_scales[PLANES * c : PLANES * (c + 1), 4 * quad : 4 * quad + 4, :].bitcast(F32),
+                )
 
         def weight_plane(g, cols):
             first = 4 * (g % PLANES)
@@ -177,8 +182,8 @@ def tile_layernormlstmcell_k_kernel(
         x_codes = keep.tile([P, GROUPS, P], U32, name="x_codes", align_bytes=64)
         x_planes = keep.tile([P, GROUPS, P], U8, name="x_planes", align_bytes=64)
 
-        def transpose_pair(source_words, first_group, n_groups, grouped, engine_copy):
-            flipped = banks.tile([P, n_groups, 2, P], F32, name="flipped", tag="bank")
+        def transpose_groups(source_words, first_group, n_groups, bank):
+            flipped = banks.tile([P, n_groups, 2, P], F32, name="flipped", tag=bank)
             for i in range(n_groups):
                 base = (first_group + i) * (K_PASS // 2)
                 for u in range(2):
@@ -187,26 +192,34 @@ def tile_layernormlstmcell_k_kernel(
                         source_words[:, base + u : base + K_PASS // 2 : 2],
                         ident_f32[:],
                     )
+            return flipped
+
+        def regroup(engine_copy, grouped, flipped):
             engine_copy(out=grouped.bitcast(F32), in_=flipped[:].rearrange("p g u r -> p g r u"))
 
-        x_words = x_sb[:].bitcast(F32)
-        for c in range(X_GROUPS // CHUNK):
-            grouped = stage.tile([P, CHUNK, P, PACK], BF16, name="grouped", align_bytes=64)
-            transpose_pair(x_words, CHUNK * c, 2, grouped[:, 0:2, :, :], nc.vector.tensor_copy)
-            transpose_pair(x_words, CHUNK * c + 2, 2, grouped[:, 2:4, :, :], nc.scalar.copy)
-            groups = slice(CHUNK * c, CHUNK * (c + 1))
+        def quantise(groups, grouped):
             nc.vector.quantize_mx(
                 out=x_codes[:, groups, :].rearrange("p g r -> p (g r)").bitcast(FP8X4),
                 scales=x_planes[:, groups, :].rearrange("p g r -> p (g r)"),
                 in_=grouped[:].rearrange("p g r t -> p (g r t)"),
             )
+
+        x_words = x_sb[:].bitcast(F32)
+        waiting = []
+        for c in range(X_GROUPS // CHUNK):
+            grouped = stage.tile([P, CHUNK, P, PACK], BF16, name="grouped", align_bytes=64)
+            first = CHUNK * c
+            left = transpose_groups(x_words, first, 2, "bank%d" % (2 * c))
+            right = transpose_groups(x_words, first + 2, 2, "bank%d" % (2 * c + 1))
+            regroup(nc.vector.tensor_copy, grouped[:, 0:2, :, :], left)
+            regroup(nc.scalar.copy, grouped[:, 2:4, :, :], right)
+            if waiting:
+                quantise(*waiting.pop())
+            waiting.append((slice(first, first + CHUNK), grouped))
         grouped_h = stage.tile([P, 1, P, PACK], BF16, name="grouped_h", align_bytes=64)
-        transpose_pair(hx_sb[:].bitcast(F32), 0, 1, grouped_h[:], nc.vector.tensor_copy)
-        nc.vector.quantize_mx(
-            out=x_codes[:, H_GROUP, :].bitcast(FP8X4),
-            scales=x_planes[:, H_GROUP, :],
-            in_=grouped_h[:].rearrange("p g r t -> p (g r t)"),
-        )
+        regroup(nc.vector.tensor_copy, grouped_h[:], transpose_groups(hx_sb[:].bitcast(F32), 0, 1, "bank5"))
+        quantise(*waiting.pop())
+        quantise(slice(H_GROUP, GROUPS), grouped_h)
 
         def mx_pass(acc, g, w_words, cols, start, stop):
             nc.tensor.matmul_mx(
@@ -219,32 +232,22 @@ def tile_layernormlstmcell_k_kernel(
                 stop=stop,
             )
 
-        both_shifts = small.tile([P, 1], BF16, name="both_shifts")
-        nc.vector.tensor_add(
-            out=both_shifts[:],
-            in0=ident_bf16[:, ROW_S_I2H : ROW_S_I2H + 1],
-            in1=ident_bf16[:, ROW_S_H2H : ROW_S_H2H + 1],
-        )
+        order = ["bank6", "bank7", "bank5"]
+
+        def next_bank():
+            order.append(order[0])
+            return order.pop(0)
 
         def spread(pick, width, label):
             wide = keep.tile([P, width], F32, name=label)
             for first in range(0, width, HID):
                 cols = slice(first, first + HID)
-                bank = banks.tile([P, HID], F32, name="bank", tag="bank")
+                bank = banks.tile([P, HID], F32, name="bank", tag=next_bank())
                 nc.tensor.matmul(
                     bank[:], lhsT=pick.to_broadcast([P, P]), rhs=rows[:, cols], start=True, stop=True
                 )
                 nc.scalar.copy(out=wide[:, cols], in_=bank[:])
             return wide
-
-        bias_h2h = spread(ident_bf16[:, ROW_B_H2H : ROW_B_H2H + 1], WIDE, "bias_h2h")
-        gain_h2h = spread(ident_bf16[:, ROW_W_H2H : ROW_W_H2H + 1], WIDE, "gain_h2h")
-        shift = spread(both_shifts[:], WIDE, "shift")
-        bias_i2h = spread(ident_bf16[:, ROW_B_I2H : ROW_B_I2H + 1], WIDE, "bias_i2h")
-        gain_i2h = spread(ident_bf16[:, ROW_W_I2H : ROW_W_I2H + 1], WIDE, "gain_i2h")
-        h2o = spread(ident_bf16[:, ROW_H2O : ROW_H2O + 1], 2 * HID, "h2o")
-        gain_h2o = h2o[:, 0:HID]
-        shift_h2o = h2o[:, HID : 2 * HID]
 
         gate_cols = [slice(j * HID, (j + 1) * HID) for j in range(GATES)]
 
@@ -252,69 +255,122 @@ def tile_layernormlstmcell_k_kernel(
         nc.sync.dma_start(
             out=w_h[:].bitcast(I32), in_=w_h2h_words[0].rearrange("p n t -> p (n t)").bitcast(I32)
         )
+        bias_h2h = spread(ident_bf16[:, ROW_B_H2H : ROW_B_H2H + 1], WIDE, "bias_h2h")
+        gain_h2h = spread(ident_bf16[:, ROW_W_H2H : ROW_W_H2H + 1], WIDE, "gain_h2h")
+        shift = spread(both_shifts[:], WIDE, "shift")
         h2h = keep.tile([P, WIDE], F32, name="h2h")
         stats_h2h = small.tile([P, GATES, 6], F32, name="stats_h2h")
         for j in range(GATES):
-            bank = banks.tile([P, HID], F32, name="bank", tag="bank")
+            bank = banks.tile([P, HID], F32, name="bank", tag=next_bank())
             mx_pass(bank[:], H_GROUP, w_h[:, gate_cols[j]], gate_cols[j], True, True)
             nc.vector.tensor_add(out=h2h[:, gate_cols[j]], in0=bank[:], in1=bias_h2h[:, gate_cols[j]])
-            nc.vector.bn_stats(out=stats_h2h[:, j, :], in_=h2h[:, gate_cols[j]])
+            if j > 0:
+                nc.vector.bn_stats(out=stats_h2h[:, j - 1, :], in_=h2h[:, gate_cols[j - 1]])
+        nc.vector.bn_stats(out=stats_h2h[:, GATES - 1, :], in_=h2h[:, gate_cols[GATES - 1]])
         mean_h, root_h = mean_and_root(nc, small, stats_h2h[:].rearrange("p c s -> p (c s)"), half, "h2h")
-        rstd_h = one_over(nc, small, unbiased_std_plus_eps(nc, small, root_h, WIDE, "h2h"), "h2h")
         for j in range(GATES):
             cols = gate_cols[j]
             centre_times_gain(nc, h2h[:, cols], h2h[:, cols], mean_h, gain_h2h[:, cols])
+        rstd_h = one_over(nc, small, unbiased_std_plus_eps(nc, small, root_h, WIDE, "h2h"), "h2h")
+        for j in range(GATES):
+            cols = gate_cols[j]
             times_scalar_plus(nc, shift[:, cols], h2h[:, cols], rstd_h, shift[:, cols])
 
-        acc = [sums.tile([P, HID], F32, name="acc%d" % j) for j in range(GATES)]
-        for g in range(MAIN):
+        load_row(ROW_B_I2H, b_i2h.rearrange("(o n) -> o n", o=1))
+        load_row(ROW_W_I2H, ln_i2h_w)
+        load_row(ROW_H2O, ln_h2o_w)
+        load_row(ROW_H2O, ln_h2o_b, HID)
+        cx_sb = keep.tile([P, HID], BF16, name="cx_sb")
+        nc.scalar.dma_start(out=cx_sb[:], in_=cx[:, :])
+
+        spans = [(GATE_I * HID, HID), (GATE_F * HID, HID), (GATE_C * HID, HID)]
+        spans += [(GATE_O * HID + h * HALF, HALF) for h in range(2)]
+        acc = {
+            first: banks.tile([P, width], F32, name="acc_%d" % first, tag="bank%d" % i)
+            for i, (first, width) in enumerate(spans)
+        }
+
+        def whole_group(g):
             w_g = weights.tile([P, WIDE], U32, name="w_g", tag="w", align_bytes=64)
             nc.sync.dma_start(
                 out=w_g[:].bitcast(I32), in_=w_i2h_words[g].rearrange("p n t -> p (n t)").bitcast(I32)
             )
-            for j in range(GATES):
-                mx_pass(acc[j][:], g, w_g[:, gate_cols[j]], gate_cols[j], g == 0, False)
-        stack.enter_context(tc.manual_schedule())
+            for first, width in spans:
+                cols = slice(first, first + width)
+                mx_pass(acc[first][:], g, w_g[:, cols], cols, g == 0, False)
+
+        whole_group(0)
+        whole_group(1)
+        bias_i2h = spread(ident_bf16[:, ROW_B_I2H : ROW_B_I2H + 1], WIDE, "bias_i2h")
+        whole_group(2)
+        gain_i2h = spread(ident_bf16[:, ROW_W_I2H : ROW_W_I2H + 1], WIDE, "gain_i2h")
+        whole_group(3)
+        h2o = spread(ident_bf16[:, ROW_H2O : ROW_H2O + 1], 2 * HID, "h2o")
+        gain_h2o = h2o[:, 0:HID]
+        shift_h2o = h2o[:, HID : 2 * HID]
+        for g in range(4, MAIN):
+            whole_group(g)
 
         i2h = keep.tile([P, WIDE], F32, name="i2h")
-        stats_i2h = small.tile([P, GATES, 2, 6], F32, name="stats_i2h")
+        stats_i2h = small.tile([P, WIDE // HALF, 6], F32, name="stats_i2h")
         halves = [slice(0, HALF), slice(HALF, HID)]
-        for j in range(GATES):
-            cols = gate_cols[j]
-            for first in range(MAIN, X_GROUPS, PIECE):
-                w_j = weights.tile([P, PIECE, HID], U32, name="w_j", tag="w", align_bytes=64)
+
+        def last_piece(*piece):
+            first_col = piece[0][0]
+            width = sum(span[1] for span in piece)
+            for g in range(MAIN, X_GROUPS, PIECE):
+                w_j = weights.tile([P, PIECE, width], U32, name="w_j", tag="w", align_bytes=64)
                 nc.sync.dma_start(
                     out=w_j[:].bitcast(I32),
-                    in_=w_i2h_words[first : first + PIECE, :, cols, :]
+                    in_=w_i2h_words[g : g + PIECE, :, first_col : first_col + width, :]
                     .rearrange("g p n t -> p g (n t)")
                     .bitcast(I32),
                 )
                 for i in range(PIECE):
-                    mx_pass(acc[j][:], first + i, w_j[:, i, :], cols, False, first + i == X_GROUPS - 1)
-            for part in halves:
+                    for first, n in piece:
+                        at = first - first_col
+                        mx_pass(
+                            acc[first][:],
+                            g + i,
+                            w_j[:, i, at : at + n],
+                            slice(first, first + n),
+                            False,
+                            g + i == X_GROUPS - 1,
+                        )
+            starts = [(first, col) for first, n in piece for col in range(first, first + n, HALF)]
+            for first, col in starts:
                 nc.vector.tensor_add(
-                    out=i2h[:, cols][:, part], in0=acc[j][:, part], in1=bias_i2h[:, cols][:, part]
+                    out=i2h[:, col : col + HALF],
+                    in0=acc[first][:, col - first : col - first + HALF],
+                    in1=bias_i2h[:, col : col + HALF],
                 )
-            for h in range(2):
-                nc.vector.bn_stats(out=stats_i2h[:, j, h, :], in_=i2h[:, cols][:, halves[h]])
+            for first, col in starts:
+                nc.vector.bn_stats(
+                    out=stats_i2h[:, col // HALF, :], in_=i2h[:, col : col + HALF]
+                )
+
+        last_piece(spans[0], spans[1])
+        last_piece(spans[2])
+        last_piece(spans[3])
+        last_piece(spans[4])
 
         gate = keep.tile([P, WIDE], F32, name="gate")
 
-        def gate_centre(j):
-            cols = gate_cols[j]
+        def gate_centre(j, part=slice(0, HID)):
+            cols = slice(j * HID + part.start, j * HID + part.stop)
             centre_times_gain(nc, gate[:, cols], i2h[:, cols], mean_i, gain_i2h[:, cols])
 
         def gate_add_shift(j):
             cols = gate_cols[j]
             times_scalar_plus(nc, gate[:, cols], shift[:, cols], std_i, gate[:, cols])
 
-        mean_i, root_i = mean_and_root(nc, small, stats_i2h[:].rearrange("p c h s -> p (c h s)"), half, "i2h")
+        mean_i, root_i = mean_and_root(nc, small, stats_i2h[:].rearrange("p c s -> p (c s)"), half, "i2h")
         gate_centre(GATE_F)
         gate_centre(GATE_I)
-        gate_centre(GATE_C)
         std_i = unbiased_std_plus_eps(nc, small, root_i, WIDE, "i2h")
-        gate_add_shift(GATE_F)
+        gate_centre(GATE_C)
         rstd_i = one_over(nc, small, std_i, "i2h")
+        gate_add_shift(GATE_F)
         gate_add_shift(GATE_I)
         gate_add_shift(GATE_C)
         forget = gate[:, gate_cols[GATE_F]]
@@ -322,11 +378,12 @@ def tile_layernormlstmcell_k_kernel(
         take_in = gate[:, gate_cols[GATE_I]]
         nc.scalar.activation(out=take_in, in_=take_in, func=ACT.Sigmoid, scale=rstd_i)
         candidate = gate[:, gate_cols[GATE_C]]
-        nc.scalar.activation(out=candidate, in_=candidate, func=ACT.Tanh, scale=rstd_i)
+        for part in halves:
+            nc.scalar.activation(out=candidate[:, part], in_=candidate[:, part], func=ACT.Tanh, scale=rstd_i)
 
         kept = keep.tile([P, HID], F32, name="kept")
         nc.vector.tensor_mul(out=kept[:], in0=forget, in1=cx_sb[:])
-        gate_centre(GATE_O)
+        gate_centre(GATE_O, halves[0])
         fresh = keep.tile([P, HID], F32, name="fresh")
         for part in halves:
             nc.vector.tensor_mul(out=fresh[:, part], in0=take_in[:, part], in1=candidate[:, part])
@@ -339,9 +396,10 @@ def tile_layernormlstmcell_k_kernel(
         nc.sync.dma_start(out=out_1[:, :], in_=cx_new[:])
 
         mean_c, root_c = mean_and_root(nc, small, stats_c[:].rearrange("p h s -> p (h s)"), half, "h2o")
+        gate_centre(GATE_O, halves[1])
+        gate_add_shift(GATE_O)
         cell = keep.tile([P, HID], F32, name="cell")
         centre_times_gain(nc, cell[:], cx_new[:], mean_c, gain_h2o)
-        gate_add_shift(GATE_O)
         let_out = gate[:, gate_cols[GATE_O]]
         nc.scalar.activation(out=let_out, in_=let_out, func=ACT.Sigmoid, scale=rstd_i)
         std_c = unbiased_std_plus_eps(nc, small, root_c, HID, "h2o")

@@ -146,10 +146,8 @@ def tile_layernormlstmcell_k_kernel(
         )
 
         x_sb = keep.tile([P, IN], BF16, name="x_sb")
-        chunk_cols = CHUNK * K_PASS
-        for c in range(X_GROUPS // CHUNK):
-            cols = slice(c * chunk_cols, (c + 1) * chunk_cols)
-            nc.sync.dma_start(out=x_sb[:, cols], in_=inputs[:, cols])
+        for half_x in (slice(0, IN // 2), slice(IN // 2, IN)):
+            nc.sync.dma_start(out=x_sb[:, half_x], in_=inputs[:, half_x])
         hx_sb = keep.tile([P, HID], BF16, name="hx_sb")
         nc.sync.dma_start(out=hx_sb[:], in_=hx[:, :])
 
@@ -280,8 +278,6 @@ def tile_layernormlstmcell_k_kernel(
         load_row(ROW_W_I2H, ln_i2h_w)
         load_row(ROW_H2O, ln_h2o_w)
         load_row(ROW_H2O, ln_h2o_b, HID)
-        cx_sb = keep.tile([P, HID], BF16, name="cx_sb")
-        nc.scalar.dma_start(out=cx_sb[:], in_=cx[:, :])
 
         spans = [(GATE_I * HID, HID), (GATE_F * HID, HID), (GATE_C * HID, HID)]
         spans += [(GATE_O * HID + h * HALF, HALF) for h in range(2)]
@@ -353,6 +349,8 @@ def tile_layernormlstmcell_k_kernel(
         last_piece(spans[2])
         last_piece(spans[3])
         last_piece(spans[4])
+        cx_sb = keep.tile([P, HID], BF16, name="cx_sb")
+        nc.sync.dma_start(out=cx_sb[:], in_=cx[:, :])
 
         gate = keep.tile([P, WIDE], F32, name="gate")
 

@@ -167,7 +167,7 @@ def tile_layernormlstmcell_k_kernel(
                 in_=w_h2h_scales[0, 4 * quad : 4 * quad + 4, :].bitcast(F32),
             )
         for c in range(X_GROUPS // PLANES):
-            for quad in (0, 2, 1, 3):
+            for quad in range(4):
                 nc.gpsimd.dma_start(
                     out=planes_f32[32 * quad : 32 * quad + 4 * PLANES, c, :],
                     in_=w_i2h_scales[PLANES * c : PLANES * (c + 1), 4 * quad : 4 * quad + 4, :].bitcast(F32),

@@ -37,13 +37,13 @@ PIECE = 2
 HALF = HID // 2
 MAIN = X_GROUPS - LAST
 
-ROW_B_I2H = 0
-ROW_W_I2H = 1
-ROW_S_I2H = 2
-ROW_S_H2H = 3
-ROW_B_H2H = 4
-ROW_W_H2H = 5
-ROW_H2O = 6
+ROW_B_I2H = 16
+ROW_W_I2H = 20
+ROW_S_I2H = 24
+ROW_S_H2H = 28
+ROW_B_H2H = 80
+ROW_W_H2H = 84
+ROW_H2O = 88
 
 FLOPS = 2 * P * (IN + HID) * WIDE
 

@@ -121,7 +121,7 @@ def tile_layernormlstmcell_k_kernel(
         forget_bias = small.tile([P, 1], F32, name="forget_bias")
         nc.vector.memset(forget_bias[:], FORGET_GATE_BIAS)
         warm = small.tile([P, 1], F32, name="warm")
-        nc.scalar.activation(out=warm[:], in_=forget_bias[:], func=ACT.Sigmoid)
+        nc.scalar.activation(out=warm[:], in_=half[:], func=ACT.Sqrt)
 
         w_planes = keep.tile([P, GROUPS // PLANES + 1, WIDE], U8, name="w_planes", align_bytes=64)
         rows = keep.tile([P, WIDE], BF16, name="rows")
@@ -136,6 +136,8 @@ def tile_layernormlstmcell_k_kernel(
 
         ident_f32 = keep.tile([P, P], F32, name="ident_f32")
         make_identity(nc, ident_f32[:])
+        minus_ident = keep.tile([P, P], F32, name="minus_ident")
+        nc.vector.tensor_scalar_mul(minus_ident[:], ident_f32[:], -1.0)
         ident_bf16 = keep.tile([P, P], BF16, name="ident_bf16")
         make_identity(nc, ident_bf16[:])
         both_shifts = small.tile([P, 1], BF16, name="both_shifts")
@@ -279,8 +281,8 @@ def tile_layernormlstmcell_k_kernel(
         load_row(ROW_H2O, ln_h2o_w)
         load_row(ROW_H2O, ln_h2o_b, HID)
 
-        spans = [(GATE_I * HID, HID), (GATE_F * HID, HID), (GATE_C * HID, HID)]
-        spans += [(GATE_O * HID + h * HALF, HALF) for h in range(2)]
+        spans = [(GATE_O * HID, HID), (GATE_C * HID, HID), (GATE_I * HID, HID)]
+        spans += [(GATE_F * HID + h * HALF, HALF) for h in range(2)]
         acc = {
             first: banks.tile([P, width], F32, name="acc_%d" % first, tag="bank%d" % i)
             for i, (first, width) in enumerate(spans)
@@ -301,17 +303,28 @@ def tile_layernormlstmcell_k_kernel(
         whole_group(2)
         gain_i2h = spread(ident_bf16[:, ROW_W_I2H : ROW_W_I2H + 1], WIDE, "gain_i2h")
         whole_group(3)
-        h2o = spread(ident_bf16[:, ROW_H2O : ROW_H2O + 1], 2 * HID, "h2o")
-        gain_h2o = h2o[:, 0:HID]
-        shift_h2o = h2o[:, HID : 2 * HID]
+        pick_h2o = ident_bf16[:, ROW_H2O : ROW_H2O + 1]
+        gain_h2o = banks.tile([P, HID], F32, name="gain_h2o", tag="bank6")
+        shift_bank = banks.tile([P, HID], F32, name="shift_bank", tag="bank7")
+        for first, bank in ((0, gain_h2o), (HID, shift_bank)):
+            nc.tensor.matmul(
+                bank[:],
+                lhsT=pick_h2o.to_broadcast([P, P]),
+                rhs=rows[:, first : first + HID],
+                start=True,
+                stop=True,
+            )
+        shift_h2o = keep.tile([P, HID], F32, name="shift_h2o")
+        nc.scalar.copy(out=shift_h2o[:], in_=shift_bank[:])
         for g in range(4, MAIN):
             whole_group(g)
 
         i2h = keep.tile([P, WIDE], F32, name="i2h")
-        stats_i2h = small.tile([P, WIDE // HALF, 6], F32, name="stats_i2h")
+        stats_i2h = small.tile([P, WIDE // HALF + 1, 6], F32, name="stats_i2h")
+        counted = []
         halves = [slice(0, HALF), slice(HALF, HID)]
 
-        def last_piece(*piece):
+        def last_piece(*piece, step=HALF):
             first_col = piece[0][0]
             width = sum(span[1] for span in piece)
             for g in range(MAIN, X_GROUPS, PIECE):
@@ -333,22 +346,30 @@ def tile_layernormlstmcell_k_kernel(
                             False,
                             g + i == X_GROUPS - 1,
                         )
-            starts = [(first, col) for first, n in piece for col in range(first, first + n, HALF)]
+            starts = [(first, col) for first, n in piece for col in range(first, first + n, step)]
             for first, col in starts:
                 nc.vector.tensor_add(
-                    out=i2h[:, col : col + HALF],
-                    in0=acc[first][:, col - first : col - first + HALF],
-                    in1=bias_i2h[:, col : col + HALF],
+                    out=i2h[:, col : col + step],
+                    in0=acc[first][:, col - first : col - first + step],
+                    in1=bias_i2h[:, col : col + step],
                 )
             for first, col in starts:
-                nc.vector.bn_stats(
-                    out=stats_i2h[:, col // HALF, :], in_=i2h[:, col : col + HALF]
-                )
+                nc.vector.bn_stats(out=stats_i2h[:, len(counted), :], in_=i2h[:, col : col + step])
+                counted.append(col)
+
+        cols_o = gate_cols[GATE_O]
+        gained_o = keep.tile([P, HID], F32, name="gained_o")
+        sum_o = banks.tile([P, HID], F32, name="sum_o", tag="bank5")
+
+        def add_to_sum_o(diagonal, columns, start, stop):
+            nc.tensor.matmul(sum_o[:], lhsT=diagonal[:], rhs=columns, start=start, stop=stop)
 
         last_piece(spans[0], spans[1])
+        nc.gpsimd.tensor_tensor(out=gained_o[:], in0=i2h[:, cols_o], in1=gain_i2h[:, cols_o], op=ALU.mult)
         last_piece(spans[2])
         last_piece(spans[3])
-        last_piece(spans[4])
+        last_piece(spans[4], step=HALF // 2)
+        add_to_sum_o(ident_f32, gained_o[:], True, False)
         cx_sb = keep.tile([P, HID], BF16, name="cx_sb")
         nc.sync.dma_start(out=cx_sb[:], in_=cx[:, :])
 
@@ -358,19 +379,33 @@ def tile_layernormlstmcell_k_kernel(
             cols = slice(j * HID + part.start, j * HID + part.stop)
             centre_times_gain(nc, gate[:, cols], i2h[:, cols], mean_i, gain_i2h[:, cols])
 
-        def gate_add_shift(j):
-            cols = gate_cols[j]
-            times_scalar_plus(nc, gate[:, cols], shift[:, cols], std_i, gate[:, cols])
+        def gate_add_shift(j, part=slice(0, HID)):
+            cols = slice(j * HID + part.start, j * HID + part.stop)
+            times_scalar_plus(nc, gate[:, cols], shift[:, cols], std_i[:], gate[:, cols])
 
-        mean_i, root_i = mean_and_root(nc, small, stats_i2h[:].rearrange("p c s -> p (c s)"), half, "i2h")
+        mean_var_i = small.tile([P, 2], F32, name="mean_var_i2h")
+        nc.vector.bn_aggr(out=mean_var_i[:], in_=stats_i2h[:].rearrange("p c s -> p (c s)"))
+        mean_i = mean_var_i[:, 0:1]
+        root_i = small.tile([P, 1], F32, name="root_i2h")
+        nc.scalar.activation(out=root_i[:], in_=mean_var_i[:, 1:2], func=ACT.Sqrt, scale=WIDE / (WIDE - 1.0))
+        diag_mean = small.tile([P, P], F32, name="diag_mean")
+        nc.scalar.activation(out=diag_mean[:], in_=minus_ident[:], func=ACT.Copy, scale=mean_i)
+        add_to_sum_o(diag_mean, gain_i2h[:, cols_o], False, False)
+        nc.scalar.activation(out=warm[:], in_=half[:], func=ACT.Sigmoid)
         gate_centre(GATE_F)
+        std_i = small.tile([P, 1], F32, name="std_eps_i2h")
+        nc.vector.tensor_scalar_add(std_i[:], root_i[:], EPS)
+        diag_std = small.tile([P, P], F32, name="diag_std")
+        nc.scalar.activation(out=diag_std[:], in_=ident_f32[:], func=ACT.Copy, scale=std_i[:])
+        add_to_sum_o(diag_std, shift[:, cols_o], False, True)
         gate_centre(GATE_I)
-        std_i = unbiased_std_plus_eps(nc, small, root_i, WIDE, "i2h")
-        gate_centre(GATE_C)
-        rstd_i = one_over(nc, small, std_i, "i2h")
+        rstd_i = one_over(nc, small, std_i[:], "i2h")
         gate_add_shift(GATE_F)
         gate_add_shift(GATE_I)
-        gate_add_shift(GATE_C)
+        gate_centre(GATE_C, halves[0])
+        gate_centre(GATE_C, halves[1])
+        gate_add_shift(GATE_C, halves[0])
+        gate_add_shift(GATE_C, halves[1])
         forget = gate[:, gate_cols[GATE_F]]
         nc.scalar.activation(out=forget, in_=forget, func=ACT.Sigmoid, scale=rstd_i, bias=forget_bias[:])
         take_in = gate[:, gate_cols[GATE_I]]
@@ -381,7 +416,6 @@ def tile_layernormlstmcell_k_kernel(
 
         kept = keep.tile([P, HID], F32, name="kept")
         nc.vector.tensor_mul(out=kept[:], in0=forget, in1=cx_sb[:])
-        gate_centre(GATE_O, halves[0])
         fresh = keep.tile([P, HID], F32, name="fresh")
         for part in halves:
             nc.vector.tensor_mul(out=fresh[:, part], in0=take_in[:, part], in1=candidate[:, part])
@@ -394,19 +428,23 @@ def tile_layernormlstmcell_k_kernel(
         nc.sync.dma_start(out=out_1[:, :], in_=cx_new[:])
 
         mean_c, root_c = mean_and_root(nc, small, stats_c[:].rearrange("p h s -> p (h s)"), half, "h2o")
-        gate_centre(GATE_O, halves[1])
-        gate_add_shift(GATE_O)
         cell = keep.tile([P, HID], F32, name="cell")
-        centre_times_gain(nc, cell[:], cx_new[:], mean_c, gain_h2o)
-        let_out = gate[:, gate_cols[GATE_O]]
-        nc.scalar.activation(out=let_out, in_=let_out, func=ACT.Sigmoid, scale=rstd_i)
+        centre_times_gain(nc, cell[:], cx_new[:], mean_c, gain_h2o[:])
+        let_out = gate[:, cols_o]
+        nc.scalar.activation(out=let_out, in_=sum_o[:], func=ACT.Sigmoid, scale=rstd_i)
         std_c = unbiased_std_plus_eps(nc, small, root_c, HID, "h2o")
-        times_scalar_plus(nc, cell[:, halves[0]], shift_h2o[:, halves[0]], std_c, cell[:, halves[0]])
+        pieces = [slice(0, 128), slice(128, 384), slice(384, HID)]
+
+        def cell_add_shift(part):
+            times_scalar_plus(nc, cell[:, part], shift_h2o[:, part], std_c, cell[:, part])
+
+        cell_add_shift(pieces[0])
         rstd_c = one_over(nc, small, std_c, "h2o")
-        times_scalar_plus(nc, cell[:, halves[1]], shift_h2o[:, halves[1]], std_c, cell[:, halves[1]])
+        cell_add_shift(pieces[1])
+        cell_add_shift(pieces[2])
         hx_new = keep.tile([P, HID], F32, name="hx_new")
-        for part in halves:
+        for part in pieces:
             nc.scalar.activation(out=cell[:, part], in_=cell[:, part], func=ACT.Tanh, scale=rstd_c)
-        for part in halves:
             nc.vector.tensor_mul(out=hx_new[:, part], in0=let_out[:, part], in1=cell[:, part])
+        for part in (slice(0, 384), slice(384, HID)):
             nc.sync.dma_start(out=out_0[:, part], in_=hx_new[:, part])

import math
from contextlib import ExitStack

import concourse.mybir as mybir
from concourse.masks import make_identity

F32 = mybir.dt.float32
BF16 = mybir.dt.bfloat16
I32 = mybir.dt.int32
U32 = mybir.dt.uint32
U8 = mybir.dt.uint8
FP8X4 = mybir.dt.float8_e4m3fn_x4
ALU = mybir.AluOpType
ACT = mybir.ActivationFunctionType

P = 128
PACK = 4
K_PASS = P * PACK
IN = 8192
HID = 512
GATES = 4
WIDE = GATES * HID
GATE_I = 0
GATE_F = 1
GATE_O = 2
GATE_C = 3
FORGET_GATE_BIAS = -1.0
EPS = 1e-5

X_GROUPS = IN // K_PASS
H_GROUP = X_GROUPS
GROUPS = X_GROUPS + 1
CHUNK = 4
PLANES = 4
LAST = 4
PIECE = 2
HALF = HID // 2
MAIN = X_GROUPS - LAST

ROW_B_I2H = 16
ROW_W_I2H = 20
ROW_S_I2H = 24
ROW_S_H2H = 28
ROW_B_H2H = 80
ROW_W_H2H = 84
ROW_H2O = 88

FLOPS = 2 * P * (IN + HID) * WIDE


def mean_and_root(nc, small, stats, half, label):
    mean_var = small.tile([P, 2], F32, name="mean_var_" + label)
    nc.vector.bn_aggr(out=mean_var[:], in_=stats)
    root = small.tile([P, 1], F32, name="root_" + label)
    nc.gpsimd.tensor_tensor(out=root[:], in0=mean_var[:, 1:2], in1=half[:], op=ALU.pow)
    return mean_var[:, 0:1], root[:]


def unbiased_std_plus_eps(nc, small, root, count, label):
    std_eps = small.tile([P, 1], F32, name="std_eps_" + label)
    nc.vector.tensor_scalar(
        out=std_eps[:],
        in0=root,
        scalar1=math.sqrt(count / (count - 1.0)),
        scalar2=EPS,
        op0=ALU.mult,
        op1=ALU.add,
    )
    return std_eps[:]


def one_over(nc, small, value, label):
    inverse = small.tile([P, 1], F32, name="inverse_" + label)
    nc.vector.reciprocal(out=inverse[:], in_=value)
    return inverse[:]


def centre_times_gain(nc, out, value, mean, gain):
    nc.vector.scalar_tensor_tensor(
        out=out, in0=value, scalar=mean, in1=gain, op0=ALU.subtract, op1=ALU.mult
    )


def times_scalar_plus(nc, out, value, scalar, other):
    nc.vector.scalar_tensor_tensor(
        out=out, in0=value, scalar=scalar, in1=other, op0=ALU.mult, op1=ALU.add
    )


def tile_layernormlstmcell_k_kernel(
    tc,
    inputs,
    hx,
    cx,
    w_i2h_words,
    w_i2h_scales,
    b_i2h,
    w_h2h_words,
    w_h2h_scales,
    b_h2h,
    ln_i2h_w,
    ln_i2h_b,
    ln_h2h_w,
    ln_h2h_b,
    ln_h2o_w,
    ln_h2o_b,
    out_0,
    out_1,
):
    nc = tc.nc
    with ExitStack() as stack:
        keep = stack.enter_context(tc.tile_pool(name="keep", bufs=1))
        small = stack.enter_context(tc.tile_pool(name="small", bufs=1))
        stage = stack.enter_context(tc.tile_pool(name="stage", bufs=2))
        weights = stack.enter_context(tc.tile_pool(name="weights", bufs=8))
        banks = stack.enter_context(tc.psum_pool(name="banks", bufs=1))
        stack.enter_context(tc.manual_schedule())

        half = small.tile([P, 1], F32, name="half")
        nc.vector.memset(half[:], 0.5)
        forget_bias = small.tile([P, 1], F32, name="forget_bias")
        nc.vector.memset(forget_bias[:], FORGET_GATE_BIAS)
        warm = small.tile([P, 1], F32, name="warm")
        nc.scalar.activation(out=warm[:], in_=half[:], func=ACT.Sqrt)

        w_planes = keep.tile([P, GROUPS // PLANES + 1, WIDE], U8, name="w_planes", align_bytes=64)
        rows = keep.tile([P, WIDE], BF16, name="rows")

        def zero_planes(c):
            nc.vector.memset(w_planes[:, c, :].bitcast(I32), 0)

        zero_planes(H_GROUP // PLANES)
        nc.vector.memset(rows[:].bitcast(I32), 0)
        for c in range(X_GROUPS // PLANES):
            zero_planes(c)

        ident_f32 = keep.tile([P, P], F32, name="ident_f32")
        make_identity(nc, ident_f32[:])
        minus_ident = keep.tile([P, P], F32, name="minus_ident")
        nc.vector.tensor_scalar_mul(minus_ident[:], ident_f32[:], -1.0)
        ident_bf16 = keep.tile([P, P], BF16, name="ident_bf16")
        make_identity(nc, ident_bf16[:])
        both_shifts = small.tile([P, 1], BF16, name="both_shifts")
        nc.vector.tensor_add(
            out=both_shifts[:],
            in0=ident_bf16[:, ROW_S_I2H : ROW_S_I2H + 1],
            in1=ident_bf16[:, ROW_S_H2H : ROW_S_H2H + 1],
        )

        x_sb = keep.tile([P, IN], BF16, name="x_sb")
        for half_x in (slice(0, IN // 2), slice(IN // 2, IN)):
            nc.sync.dma_start(out=x_sb[:, half_x], in_=inputs[:, half_x])
        hx_sb = keep.tile([P, HID], BF16, name="hx_sb")
        nc.sync.dma_start(out=hx_sb[:], in_=hx[:, :])

        def load_row(row, source, first=0):
            width = source.shape[1]
            nc.scalar.dma_start(out=rows[row : row + 1, first : first + width], in_=source)

        load_row(ROW_B_H2H, b_h2h.rearrange("(o n) -> o n", o=1))
        load_row(ROW_W_H2H, ln_h2h_w)
        load_row(ROW_S_H2H, ln_h2h_b)
        load_row(ROW_S_I2H, ln_i2h_b)

        planes_f32 = w_planes[:].bitcast(F32)
        for quad in range(4):
            nc.gpsimd.dma_start(
                out=planes_f32[32 * quad : 32 * quad + 4, H_GROUP // PLANES, :],
                in_=w_h2h_scales[0, 4 * quad : 4 * quad + 4, :].bitcast(F32),
            )
        for c in range(X_GROUPS // PLANES):
            for quad in range(4):
                nc.gpsimd.dma_start(
                    out=planes_f32[32 * quad : 32 * quad + 4 * PLANES, c, :],
                    in_=w_i2h_scales[PLANES * c : PLANES * (c + 1), 4 * quad : 4 * quad + 4, :].bitcast(F32),
                )

        def weight_plane(g, cols):
            first = 4 * (g % PLANES)
            return w_planes[first:P, g // PLANES, cols]

        x_codes = keep.tile([P, GROUPS, P], U32, name="x_codes", align_bytes=64)
        x_planes = keep.tile([P, GROUPS, P], U8, name="x_planes", align_bytes=64)

        def transpose_groups(source_words, first_group, n_groups, bank):
            flipped = banks.tile([P, n_groups, 2, P], F32, name="flipped", tag=bank)
            for i in range(n_groups):
                base = (first_group + i) * (K_PASS // 2)
                for u in range(2):
                    nc.tensor.transpose(
                        flipped[:, i, u, :],
                        source_words[:, base + u : base + K_PASS // 2 : 2],
                        ident_f32[:],
                    )
            return flipped

        def regroup(engine_copy, grouped, flipped):
            engine_copy(out=grouped.bitcast(F32), in_=flipped[:].rearrange("p g u r -> p g r u"))

        def quantise(groups, grouped):
            nc.vector.quantize_mx(
                out=x_codes[:, groups, :].rearrange("p g r -> p (g r)").bitcast(FP8X4),
                scales=x_planes[:, groups, :].rearrange("p g r -> p (g r)"),
                in_=grouped[:].rearrange("p g r t -> p (g r t)"),
            )

        x_words = x_sb[:].bitcast(F32)
        waiting = []
        for c in range(X_GROUPS // CHUNK):
            grouped = stage.tile([P, CHUNK, P, PACK], BF16, name="grouped", align_bytes=64)
            first = CHUNK * c
            left = transpose_groups(x_words, first, 2, "bank%d" % (2 * c))
            right = transpose_groups(x_words, first + 2, 2, "bank%d" % (2 * c + 1))
            regroup(nc.vector.tensor_copy, grouped[:, 0:2, :, :], left)
            regroup(nc.scalar.copy, grouped[:, 2:4, :, :], right)
            if waiting:
                quantise(*waiting.pop())
            waiting.append((slice(first, first + CHUNK), grouped))
        grouped_h = stage.tile([P, 1, P, PACK], BF16, name="grouped_h", align_bytes=64)
        regroup(nc.vector.tensor_copy, grouped_h[:], transpose_groups(hx_sb[:].bitcast(F32), 0, 1, "bank5"))
        quantise(*waiting.pop())
        quantise(slice(H_GROUP, GROUPS), grouped_h)

        def mx_pass(acc, g, w_words, cols, start, stop):
            nc.tensor.matmul_mx(
                out=acc,
                lhsT=x_codes[:, g, :].bitcast(FP8X4),
                lhsT_scale=x_planes[:, g, :],
                rhs=w_words.bitcast(FP8X4),
                rhs_scale=weight_plane(g, cols),
                start=start,
                stop=stop,
            )

        order = ["bank6", "bank7", "bank5"]

        def next_bank():
            order.append(order[0])
            return order.pop(0)

        def spread(pick, width, label):
            wide = keep.tile([P, width], F32, name=label)
            for first in range(0, width, HID):
                cols = slice(first, first + HID)
                bank = banks.tile([P, HID], F32, name="bank", tag=next_bank())
                nc.tensor.matmul(
                    bank[:], lhsT=pick.to_broadcast([P, P]), rhs=rows[:, cols], start=True, stop=True
                )
                nc.scalar.copy(out=wide[:, cols], in_=bank[:])
            return wide

        gate_cols = [slice(j * HID, (j + 1) * HID) for j in range(GATES)]

        w_h = weights.tile([P, WIDE], U32, name="w_h", tag="w", align_bytes=64)
        nc.sync.dma_start(
            out=w_h[:].bitcast(I32), in_=w_h2h_words[0].rearrange("p n t -> p (n t)").bitcast(I32)
        )
        bias_h2h = spread(ident_bf16[:, ROW_B_H2H : ROW_B_H2H + 1], WIDE, "bias_h2h")
        gain_h2h = spread(ident_bf16[:, ROW_W_H2H : ROW_W_H2H + 1], WIDE, "gain_h2h")
        shift = spread(both_shifts[:], WIDE, "shift")
        h2h = keep.tile([P, WIDE], F32, name="h2h")
        stats_h2h = small.tile([P, GATES, 6], F32, name="stats_h2h")
        for j in range(GATES):
            bank = banks.tile([P, HID], F32, name="bank", tag=next_bank())
            mx_pass(bank[:], H_GROUP, w_h[:, gate_cols[j]], gate_cols[j], True, True)
            nc.vector.tensor_add(out=h2h[:, gate_cols[j]], in0=bank[:], in1=bias_h2h[:, gate_cols[j]])
            if j > 0:
                nc.vector.bn_stats(out=stats_h2h[:, j - 1, :], in_=h2h[:, gate_cols[j - 1]])
        nc.vector.bn_stats(out=stats_h2h[:, GATES - 1, :], in_=h2h[:, gate_cols[GATES - 1]])
        mean_h, root_h = mean_and_root(nc, small, stats_h2h[:].rearrange("p c s -> p (c s)"), half, "h2h")
        for j in range(GATES):
            cols = gate_cols[j]
            centre_times_gain(nc, h2h[:, cols], h2h[:, cols], mean_h, gain_h2h[:, cols])
        rstd_h = one_over(nc, small, unbiased_std_plus_eps(nc, small, root_h, WIDE, "h2h"), "h2h")
        for j in range(GATES):
            cols = gate_cols[j]
            times_scalar_plus(nc, shift[:, cols], h2h[:, cols], rstd_h, shift[:, cols])

        load_row(ROW_B_I2H, b_i2h.rearrange("(o n) -> o n", o=1))
        load_row(ROW_W_I2H, ln_i2h_w)
        load_row(ROW_H2O, ln_h2o_w)
        load_row(ROW_H2O, ln_h2o_b, HID)

        spans = [(GATE_O * HID, HID), (GATE_C * HID, HID), (GATE_I * HID, HID)]
        spans += [(GATE_F * HID + h * HALF, HALF) for h in range(2)]
        acc = {
            first: banks.tile([P, width], F32, name="acc_%d" % first, tag="bank%d" % i)
            for i, (first, width) in enumerate(spans)
        }

        def whole_group(g):
            w_g = weights.tile([P, WIDE], U32, name="w_g", tag="w", align_bytes=64)
            nc.sync.dma_start(
                out=w_g[:].bitcast(I32), in_=w_i2h_words[g].rearrange("p n t -> p (n t)").bitcast(I32)
            )
            for first, width in spans:
                cols = slice(first, first + width)
                mx_pass(acc[first][:], g, w_g[:, cols], cols, g == 0, False)

        whole_group(0)
        whole_group(1)
        bias_i2h = spread(ident_bf16[:, ROW_B_I2H : ROW_B_I2H + 1], WIDE, "bias_i2h")
        whole_group(2)
        gain_i2h = spread(ident_bf16[:, ROW_W_I2H : ROW_W_I2H + 1], WIDE, "gain_i2h")
        whole_group(3)
        pick_h2o = ident_bf16[:, ROW_H2O : ROW_H2O + 1]
        gain_h2o = banks.tile([P, HID], F32, name="gain_h2o", tag="bank6")
        shift_bank = banks.tile([P, HID], F32, name="shift_bank", tag="bank7")
        for first, bank in ((0, gain_h2o), (HID, shift_bank)):
            nc.tensor.matmul(
                bank[:],
                lhsT=pick_h2o.to_broadcast([P, P]),
                rhs=rows[:, first : first + HID],
                start=True,
                stop=True,
            )
        shift_h2o = keep.tile([P, HID], F32, name="shift_h2o")
        nc.scalar.copy(out=shift_h2o[:], in_=shift_bank[:])
        for g in range(4, MAIN):
            whole_group(g)

        i2h = keep.tile([P, WIDE], F32, name="i2h")
        stats_i2h = small.tile([P, WIDE // HALF + 1, 6], F32, name="stats_i2h")
        counted = []
        halves = [slice(0, HALF), slice(HALF, HID)]

        def last_piece(*piece, step=HALF):
            first_col = piece[0][0]
            width = sum(span[1] for span in piece)
            for g in range(MAIN, X_GROUPS, PIECE):
                w_j = weights.tile([P, PIECE, width], U32, name="w_j", tag="w", align_bytes=64)
                nc.sync.dma_start(
                    out=w_j[:].bitcast(I32),
                    in_=w_i2h_words[g : g + PIECE, :, first_col : first_col + width, :]
                    .rearrange("g p n t -> p g (n t)")
                    .bitcast(I32),
                )
                for i in range(PIECE):
                    for first, n in piece:
                        at = first - first_col
                        mx_pass(
                            acc[first][:],
                            g + i,
                            w_j[:, i, at : at + n],
                            slice(first, first + n),
                            False,
                            g + i == X_GROUPS - 1,
                        )
            starts = [(first, col) for first, n in piece for col in range(first, first + n, step)]
            for first, col in starts:
                nc.vector.tensor_add(
                    out=i2h[:, col : col + step],
                    in0=acc[first][:, col - first : col - first + step],
                    in1=bias_i2h[:, col : col + step],
                )
            for first, col in starts:
                nc.vector.bn_stats(out=stats_i2h[:, len(counted), :], in_=i2h[:, col : col + step])
                counted.append(col)

        cols_o = gate_cols[GATE_O]
        gained_o = keep.tile([P, HID], F32, name="gained_o")
        sum_o = banks.tile([P, HID], F32, name="sum_o", tag="bank5")

        def add_to_sum_o(diagonal, columns, start, stop):
            nc.tensor.matmul(sum_o[:], lhsT=diagonal[:], rhs=columns, start=start, stop=stop)

        last_piece(spans[0], spans[1])
        nc.gpsimd.tensor_tensor(out=gained_o[:], in0=i2h[:, cols_o], in1=gain_i2h[:, cols_o], op=ALU.mult)
        last_piece(spans[2])
        last_piece(spans[3])
        last_piece(spans[4], step=HALF // 2)
        add_to_sum_o(ident_f32, gained_o[:], True, False)
        cx_sb = keep.tile([P, HID], BF16, name="cx_sb")
        nc.sync.dma_start(out=cx_sb[:], in_=cx[:, :])

        gate = keep.tile([P, WIDE], F32, name="gate")

        def gate_centre(j, part=slice(0, HID)):
            cols = slice(j * HID + part.start, j * HID + part.stop)
            centre_times_gain(nc, gate[:, cols], i2h[:, cols], mean_i, gain_i2h[:, cols])

        def gate_add_shift(j, part=slice(0, HID)):
            cols = slice(j * HID + part.start, j * HID + part.stop)
            times_scalar_plus(nc, gate[:, cols], shift[:, cols], std_i[:], gate[:, cols])

        mean_var_i = small.tile([P, 2], F32, name="mean_var_i2h")
        nc.vector.bn_aggr(out=mean_var_i[:], in_=stats_i2h[:].rearrange("p c s -> p (c s)"))
        mean_i = mean_var_i[:, 0:1]
        root_i = small.tile([P, 1], F32, name="root_i2h")
        nc.scalar.activation(out=root_i[:], in_=mean_var_i[:, 1:2], func=ACT.Sqrt, scale=WIDE / (WIDE - 1.0))
        diag_mean = small.tile([P, P], F32, name="diag_mean")
        nc.scalar.activation(out=diag_mean[:], in_=minus_ident[:], func=ACT.Copy, scale=mean_i)
        add_to_sum_o(diag_mean, gain_i2h[:, cols_o], False, False)
        nc.scalar.activation(out=warm[:], in_=half[:], func=ACT.Sigmoid)
        gate_centre(GATE_F)
        std_i = small.tile([P, 1], F32, name="std_eps_i2h")
        nc.vector.tensor_scalar_add(std_i[:], root_i[:], EPS)
        diag_std = small.tile([P, P], F32, name="diag_std")
        nc.scalar.activation(out=diag_std[:], in_=ident_f32[:], func=ACT.Copy, scale=std_i[:])
        add_to_sum_o(diag_std, shift[:, cols_o], False, True)
        gate_centre(GATE_I)
        rstd_i = one_over(nc, small, std_i[:], "i2h")
        gate_add_shift(GATE_F)
        gate_add_shift(GATE_I)
        gate_centre(GATE_C, halves[0])
        gate_centre(GATE_C, halves[1])
        gate_add_shift(GATE_C, halves[0])
        gate_add_shift(GATE_C, halves[1])
        forget = gate[:, gate_cols[GATE_F]]
        nc.scalar.activation(out=forget, in_=forget, func=ACT.Sigmoid, scale=rstd_i, bias=forget_bias[:])
        take_in = gate[:, gate_cols[GATE_I]]
        nc.scalar.activation(out=take_in, in_=take_in, func=ACT.Sigmoid, scale=rstd_i)
        candidate = gate[:, gate_cols[GATE_C]]
        for part in halves:
            nc.scalar.activation(out=candidate[:, part], in_=candidate[:, part], func=ACT.Tanh, scale=rstd_i)

        kept = keep.tile([P, HID], F32, name="kept")
        nc.vector.tensor_mul(out=kept[:], in0=forget, in1=cx_sb[:])
        fresh = keep.tile([P, HID], F32, name="fresh")
        for part in halves:
            nc.vector.tensor_mul(out=fresh[:, part], in0=take_in[:, part], in1=candidate[:, part])
        cx_new = keep.tile([P, HID], F32, name="cx_new")
        for part in halves:
            nc.vector.tensor_add(out=cx_new[:, part], in0=kept[:, part], in1=fresh[:, part])
        stats_c = small.tile([P, 2, 6], F32, name="stats_c")
        for h in range(2):
            nc.vector.bn_stats(out=stats_c[:, h, :], in_=cx_new[:, halves[h]])
        nc.sync.dma_start(out=out_1[:, :], in_=cx_new[:])

        mean_c, root_c = mean_and_root(nc, small, stats_c[:].rearrange("p h s -> p (h s)"), half, "h2o")
        cell = keep.tile([P, HID], F32, name="cell")
        centre_times_gain(nc, cell[:], cx_new[:], mean_c, gain_h2o[:])
        let_out = gate[:, cols_o]
        nc.scalar.activation(out=let_out, in_=sum_o[:], func=ACT.Sigmoid, scale=rstd_i)
        std_c = unbiased_std_plus_eps(nc, small, root_c, HID, "h2o")
        pieces = [slice(0, 128), slice(128, 384), slice(384, HID)]

        def cell_add_shift(part):
            times_scalar_plus(nc, cell[:, part], shift_h2o[:, part], std_c, cell[:, part])

        cell_add_shift(pieces[0])
        rstd_c = one_over(nc, small, std_c, "h2o")
        cell_add_shift(pieces[1])
        cell_add_shift(pieces[2])
        hx_new = keep.tile([P, HID], F32, name="hx_new")
        for part in pieces:
            nc.scalar.activation(out=cell[:, part], in_=cell[:, part], func=ACT.Tanh, scale=rstd_c)
            nc.vector.tensor_mul(out=hx_new[:, part], in0=let_out[:, part], in1=cell[:, part])
        for part in (slice(0, 384), slice(384, HID)):
            nc.sync.dma_start(out=out_0[:, part], in_=hx_new[:, part])
